import numpy as np
import ml_dtypes


def mxq(x, axis, fmt="e4m3"):
    dtype, down = {"e4m3": (ml_dtypes.float8_e4m3fn, 7), "e5m2": (ml_dtypes.float8_e5m2, 14)}[fmt]
    v = np.moveaxis(np.asarray(x, np.float32).astype(ml_dtypes.bfloat16).astype(np.float64), axis, -1)
    blocks = v.reshape(v.shape[:-1] + (-1, 32))
    amax = np.abs(blocks).max(-1, keepdims=True)
    byte = np.maximum(np.where(amax > 0, np.frexp(amax)[1] - 1 + 127, 0) - down, 1)
    scale = np.exp2(byte - 127.0)
    codes = (blocks / scale).astype(np.float32).astype(dtype).astype(np.float64)
    return np.moveaxis((codes * scale).reshape(v.shape), -1, axis)


WIDE = False


def mx_kscale(k):
    if not WIDE:
        return np.ones(k)
    levels = np.array([10, -10, 5, -5, 0])
    a = np.random.permutation(np.resize(levels, k // 512 * 4)).reshape(k // 512, 4)
    idx = np.arange(k)
    return np.exp2(a[idx // 512, idx % 128 // 32])


BF16 = ml_dtypes.bfloat16


def bf(x):
    return np.asarray(x, np.float32).astype(BF16)


def f64(x):
    return np.asarray(x).astype(np.float64)


E2M1 = np.array([0.0, 0.5, 1.0, 1.5, 2.0, 3.0, 4.0, 6.0, -0.0, -0.5, -1.0, -1.5, -2.0, -3.0, -4.0, -6.0])


def pack_weight(w, fmt):
    k, n = w.shape
    w = f64(bf(w)).reshape(k // 32, 32, n)
    amax = np.abs(w).max(1)
    if fmt == "e4m3":
        byte = np.frexp(amax)[1] - 1 + 127 - 7
    else:
        mant, ex = np.frexp(amax / 6.0)
        byte = np.where(mant > 0.5, ex, ex - 1) + 127
    byte = np.clip(np.where(amax > 0, byte, 1), 1, 254)
    scaled = (w * np.exp2(127.0 - byte)[:, None, :]).reshape(k, n).astype(np.float32)
    by_word = np.ascontiguousarray(scaled.reshape(k // 512, 128, 4, n).transpose(0, 1, 3, 2))
    if fmt == "e4m3":
        words = by_word.astype(ml_dtypes.float8_e4m3fn).view(np.uint8)
    else:
        c = by_word.astype(ml_dtypes.float4_e2m1fn).view(np.uint8) & 0xF
        words = c[..., 0::2] | (c[..., 1::2] << 4)
    return np.ascontiguousarray(words), np.ascontiguousarray(byte.astype(np.uint8).reshape(k // 512, 16, n))


def unpack_weight(words, scales, fmt):
    g, p, n, _ = words.shape
    if fmt == "e4m3":
        vals = np.ascontiguousarray(words).view(ml_dtypes.float8_e4m3fn).astype(np.float64)
    else:
        nib = np.empty((g, p, n, 4), np.uint8)
        nib[..., 0::2] = words & 0xF
        nib[..., 1::2] = words >> 4
        vals = E2M1[nib]
    vals = vals * np.repeat(np.exp2(scales.astype(np.float64) - 127.0), 8, axis=1)[..., None]
    return vals.transpose(0, 1, 3, 2).reshape(g * 512, n)


B, C, HH, WW, NH, HD, F = 2, 512, 16, 16, 8, 64, 16384
EPS = 1e-5


def layer_norm(v, w, b):
    mu = v.mean(-1, keepdims=True)
    var = ((v - mu) ** 2).mean(-1, keepdims=True)
    return (v - mu) * (1.0 / np.sqrt(var + EPS)) * w + b


def setup_inputs():
    s = mx_kscale(F)
    h = bf(np.maximum(np.random.standard_normal((B, HH, WW, F)), 0.0) * 0.125 * s)
    ffn2_w = np.random.standard_normal((C, F)) * 0.5 / np.sqrt(F) / s
    words, scales = pack_weight(np.ascontiguousarray(ffn2_w.T), "e4m3")
    return {"h": h,
            "ffn2_w_words": words,
            "ffn2_w_scales": scales,
            "ffn2_b": bf(np.random.standard_normal(C) * 0.02),
            "scale_ffn": bf(0.1 * (1.0 + 0.1 * np.random.standard_normal(1))),
            "ln2_w": bf(1.0 + 0.1 * np.random.standard_normal(C)),
            "ln2_b": bf(0.1 * np.random.standard_normal(C)),
            "scale_norm2": bf(1.5 * (1.0 + 0.1 * np.random.standard_normal(1))),
            "x": bf(np.random.standard_normal((B, C, HH, WW)))}


def reference(h, ffn2_w_words, ffn2_w_scales, ffn2_b, scale_ffn, ln2_w, ln2_b, scale_norm2, x):
    y2 = ((mxq(f64(h), 3, "e4m3") @ unpack_weight(ffn2_w_words, ffn2_w_scales, "e4m3")) + f64(ffn2_b)) * f64(scale_ffn)
    y2 = layer_norm(y2, f64(ln2_w), f64(ln2_b)) * f64(scale_norm2)
    out = np.maximum(y2 + f64(x).transpose(0, 2, 3, 1), 0.0)
    return out.transpose(0, 3, 1, 2)

@@ -1,0 +1,263 @@
+from contextlib import ExitStack
+
+import concourse.mybir as mybir
+from concourse.masks import make_identity
+
+F32 = mybir.dt.float32
+BF16 = mybir.dt.bfloat16
+I32 = mybir.dt.int32
+U32 = mybir.dt.uint32
+U8 = mybir.dt.uint8
+FP8X4 = mybir.dt.float8_e4m3fn_x4
+ALU = mybir.AluOpType
+ACT = mybir.ActivationFunctionType
+
+P = 128
+PACK = 4
+K_PASS = P * PACK
+BATCH = 2
+IMAGE = 256
+IMAGE_TILES = IMAGE // P
+PIXEL_TILES = BATCH * IMAGE_TILES
+CHANNELS = 512
+CHANNEL_TILES = CHANNELS // P
+K = 16384
+CHUNK_GROUPS = 4
+K_CHUNK = CHUNK_GROUPS * K_PASS
+CHUNKS = K // K_CHUNK
+ROUNDS = CHUNKS * BATCH
+HALVES = 2
+EPS = 1e-5
+
+H_BUFS = 10
+W_BUFS = H_BUFS // BATCH
+
+FFN_SCALE_COL = 0
+NORM_SCALE_COL = 16
+SCALAR_COLS = 32
+
+FLOPS = 2 * BATCH * IMAGE * K * CHANNELS
+
+
+def tile_transformerconvblock_pc_k_kernel(
+    tc, h, ffn2_w_words, ffn2_w_scales, ffn2_b, scale_ffn, ln2_w, ln2_b, scale_norm2, x, out
+):
+    nc = tc.nc
+    h_view = h.flatten_outer_dims().rearrange("(t p) k -> p t k", p=P)
+    w_view = ffn2_w_words.rearrange("g p n t -> p g (n t)")
+
+    with ExitStack() as ctx:
+        ctx.enter_context(tc.manual_schedule())
+        consts = ctx.enter_context(tc.tile_pool(name="consts", bufs=1))
+        h_pool = ctx.enter_context(tc.tile_pool(name="h_pool", bufs=H_BUFS))
+        w_pool = ctx.enter_context(tc.tile_pool(name="w_pool", bufs=W_BUFS))
+        work = ctx.enter_context(tc.tile_pool(name="work", bufs=2))
+        tail = ctx.enter_context(tc.tile_pool(name="tail", bufs=2))
+        acc_pool = ctx.enter_context(tc.psum_pool(name="acc_pool", bufs=1))
+        turn_pool = ctx.enter_context(tc.psum_pool(name="turn_pool", bufs=4))
+
+        h_tiles = {}
+        w_tiles = {}
+
+        def load_h(i):
+            chunk, b = divmod(i, BATCH)
+            h_rows = h_pool.tile([P, IMAGE_TILES, K_CHUNK], BF16, tag="h_rows")
+            nc.sync.dma_start(
+                out=h_rows[:],
+                in_=h_view[:, b * IMAGE_TILES : (b + 1) * IMAGE_TILES, chunk * K_CHUNK : (chunk + 1) * K_CHUNK],
+            )
+            h_tiles[i] = h_rows
+
+        def load_w(chunk):
+            w_words = w_pool.tile([P, CHUNK_GROUPS, PACK * CHANNELS], U8, tag="w_words", align_bytes=64)
+            nc.sync.dma_start(
+                out=w_words[:].bitcast(I32),
+                in_=w_view[:, chunk * CHUNK_GROUPS : (chunk + 1) * CHUNK_GROUPS, :].bitcast(I32),
+            )
+            w_tiles[chunk] = w_words
+
+        w_planes = consts.tile([P, CHUNKS, CHANNELS], U8, align_bytes=64)
+        nc.vector.memset(w_planes[:].bitcast(I32), 0)
+
+        def load_w_planes():
+            for quadrant in range(4):
+                for r in range(4):
+                    first = 32 * quadrant + r
+                    nc.sync.dma_start(
+                        out=w_planes[first : first + 4 * CHUNK_GROUPS : 4, :, :].bitcast(I32),
+                        in_=ffn2_w_scales[:, 4 * quadrant + r, :]
+                        .rearrange("(a j) n -> j a n", j=CHUNK_GROUPS)
+                        .bitcast(I32),
+                    )
+
+        load_h(0)
+        load_w(0)
+        load_w_planes()
+        for i in range(1, H_BUFS):
+            load_h(i)
+            if i % BATCH == 0:
+                load_w(i // BATCH)
+
+        x_rows = consts.tile([P, CHANNEL_TILES, BATCH, IMAGE], BF16)
+        for b in range(BATCH):
+            nc.sync.dma_start(out=x_rows[:, :, b, :], in_=x[b].rearrange("(j c) i w -> c j (i w)", c=P))
+
+        ident_f32 = consts.tile([P, P], F32)
+        make_identity(nc, ident_f32[:])
+        ident_bf16 = consts.tile([P, P], BF16)
+        make_identity(nc, ident_bf16[:])
+        ones = consts.tile([P, P], BF16)
+        nc.vector.memset(ones[:], 1.0)
+
+        one_col = consts.tile([P, 1], F32)
+        nc.vector.memset(one_col[:], 1.0)
+        sqrt_warm = consts.tile([P, 1], F32)
+        nc.scalar.activation(out=sqrt_warm[:], in_=one_col[:], func=ACT.Sqrt)
+
+        one_row = consts.tile([P, CHANNELS + SCALAR_COLS], BF16)
+        nc.vector.memset(one_row[:], 0.0)
+        nc.scalar.dma_start(out=one_row[0:1, 0:CHANNELS], in_=ffn2_b.unsqueeze(0))
+        ffn_col = CHANNELS + FFN_SCALE_COL
+        norm_col = CHANNELS + NORM_SCALE_COL
+        nc.scalar.dma_start(out=one_row[0:1, ffn_col : ffn_col + 1], in_=scale_ffn.unsqueeze(0))
+        nc.scalar.dma_start(out=one_row[0:1, norm_col : norm_col + 1], in_=scale_norm2.unsqueeze(0))
+        ln_rows = consts.tile([P, P], BF16)
+        nc.vector.memset(ln_rows[:], 0.0)
+        nc.scalar.dma_start(out=ln_rows[0:CHANNEL_TILES, :], in_=ln2_w.rearrange("(j c) -> j c", c=P))
+        nc.scalar.dma_start(
+            out=ln_rows[CHANNEL_TILES : 2 * CHANNEL_TILES, :], in_=ln2_b.rearrange("(j c) -> j c", c=P)
+        )
+
+        bias_bank = turn_pool.tile([P, CHANNELS], F32, tag="turn")
+        nc.tensor.matmul(out=bias_bank[:], lhsT=ones[:], rhs=one_row[:, 0:CHANNELS], start=True, stop=True)
+        bias_all = consts.tile([P, CHANNELS], F32)
+        nc.vector.tensor_copy(out=bias_all[:], in_=bias_bank[:])
+
+        scalar_bank = turn_pool.tile([P, SCALAR_COLS], F32, tag="turn")
+        nc.tensor.matmul(
+            out=scalar_bank[:], lhsT=ones[:], rhs=one_row[:, CHANNELS : CHANNELS + SCALAR_COLS], start=True, stop=True
+        )
+        scalars = consts.tile([P, SCALAR_COLS], F32)
+        nc.vector.tensor_copy(out=scalars[:], in_=scalar_bank[:])
+        ffn_scale = scalars[:, FFN_SCALE_COL : FFN_SCALE_COL + 1]
+        norm_scale = scalars[:, NORM_SCALE_COL : NORM_SCALE_COL + 1]
+        ffn_scale_sq = consts.tile([P, 1], F32)
+        nc.vector.tensor_tensor(out=ffn_scale_sq[:], in0=ffn_scale, in1=ffn_scale, op=ALU.mult)
+
+        ln_bank = turn_pool.tile([P, P], BF16, tag="turn")
+        nc.tensor.transpose(ln_bank[:], ln_rows[:], ident_bf16[:])
+        ln_cols = consts.tile([P, 2 * CHANNEL_TILES], F32)
+        nc.vector.tensor_scalar(
+            out=ln_cols[:], in0=ln_bank[:, 0 : 2 * CHANNEL_TILES], scalar1=norm_scale, scalar2=None, op0=ALU.mult
+        )
+
+        x_shifted = consts.tile([P, CHANNEL_TILES, BATCH, IMAGE], F32)
+        for j in range(CHANNEL_TILES):
+            nc.gpsimd.tensor_scalar(
+                out=x_shifted[:, j, :, :],
+                in0=x_rows[:, j, :, :],
+                scalar1=1.0,
+                scalar2=ln_cols[:, CHANNEL_TILES + j : CHANNEL_TILES + j + 1],
+                op0=ALU.mult,
+                op1=ALU.add,
+            )
+
+        acc = [acc_pool.tile([P, CHANNELS], F32, name="acc%d" % t) for t in range(PIXEL_TILES)]
+
+        grouped_tiles = {}
+
+        def turn(i):
+            h_words = h_tiles.pop(i)[:].bitcast(F32)
+            sorted_words = work.tile([P, IMAGE_TILES, CHUNK_GROUPS, HALVES, P], F32, tag="sorted_words")
+            nc.vector.tensor_copy(
+                out=sorted_words[:],
+                in_=h_words.rearrange("p t (g q u) -> p t g u q", g=CHUNK_GROUPS, u=HALVES),
+            )
+            if i + H_BUFS < ROUNDS:
+                load_h(i + H_BUFS)
+            grouped = work.tile([P, CHUNK_GROUPS, IMAGE * PACK], BF16, tag="grouped", align_bytes=64)
+            grouped_words = grouped[:].bitcast(F32).rearrange("p g (x u) -> p g x u", u=HALVES)
+            for g in range(CHUNK_GROUPS):
+                turned = turn_pool.tile([P, HALVES, IMAGE], F32, tag="turn")
+                for t in range(IMAGE_TILES):
+                    for u in range(HALVES):
+                        nc.tensor.transpose(turned[:, u, t * P : (t + 1) * P], sorted_words[:, t, g, u, :], ident_f32[:])
+                nc.scalar.copy(out=grouped_words[:, g, :, :], in_=turned[:].rearrange("p u x -> p x u"))
+            grouped_tiles[i] = grouped
+
+        def multiply(i):
+            chunk, b = divmod(i, BATCH)
+            grouped = grouped_tiles.pop(i)
+            h_codes = work.tile([P, CHUNK_GROUPS, IMAGE], U32, tag="h_codes", align_bytes=64)
+            h_planes = work.tile([P, CHUNK_GROUPS, IMAGE], U8, tag="h_planes", align_bytes=64)
+            for g in range(CHUNK_GROUPS):
+                nc.vector.quantize_mx(
+                    out=h_codes[:, g, :].bitcast(FP8X4), scales=h_planes[:, g, :], in_=grouped[:, g, :]
+                )
+            w_words = w_tiles[chunk]
+            for g in range(CHUNK_GROUPS):
+                for t in range(IMAGE_TILES):
+                    pixels = slice(t * P, (t + 1) * P)
+                    nc.tensor.matmul_mx(
+                        out=acc[b * IMAGE_TILES + t][:],
+                        lhsT=h_codes[:, g, pixels].bitcast(FP8X4),
+                        lhsT_scale=h_planes[:, g, pixels],
+                        rhs=w_words[:, g, :].bitcast(FP8X4),
+                        rhs_scale=w_planes[4 * g : P, chunk, :],
+                        start=(chunk == 0 and g == 0),
+                        stop=(chunk == CHUNKS - 1 and g == CHUNK_GROUPS - 1),
+                    )
+            if b == BATCH - 1 and chunk + W_BUFS < CHUNKS:
+                load_w(chunk + W_BUFS)
+
+        def finish(b):
+            normed = []
+            for t in range(IMAGE_TILES):
+                biased = tail.tile([P, CHANNELS], F32, tag="biased")
+                nc.vector.tensor_tensor(out=biased[:], in0=acc[b * IMAGE_TILES + t][:], in1=bias_all[:], op=ALU.add)
+                stats = tail.tile([P, 6], F32, tag="stats")
+                nc.vector.bn_stats(out=stats[:], in_=biased[:])
+                mean_var = tail.tile([P, 2], F32, tag="mean_var")
+                nc.vector.bn_aggr(out=mean_var[:], in_=stats[:])
+                spread = tail.tile([P, 1], F32, tag="spread")
+                nc.vector.tensor_scalar(
+                    out=spread[:], in0=mean_var[:, 1:2], scalar1=ffn_scale_sq[:], scalar2=EPS, op0=ALU.mult, op1=ALU.add
+                )
+                nc.scalar.activation(out=spread[:], in_=spread[:], func=ACT.Sqrt)
+                gain = tail.tile([P, 1], F32, tag="gain")
+                nc.vector.reciprocal(out=gain[:], in_=spread[:])
+                nc.vector.tensor_scalar(out=gain[:], in0=gain[:], scalar1=ffn_scale, scalar2=None, op0=ALU.mult)
+                unit = tail.tile([P, CHANNELS], F32, tag="unit")
+                nc.vector.tensor_scalar(
+                    out=unit[:], in0=biased[:], scalar1=mean_var[:, 0:1], scalar2=gain[:], op0=ALU.subtract, op1=ALU.mult
+                )
+                normed.append(unit)
+            out_view = out[b].rearrange("(j c) i w -> c j (i w)", c=P)
+            for pair in range(CHANNEL_TILES // 2):
+                turned = turn_pool.tile([P, 2, IMAGE], F32, tag="turn")
+                summed = tail.tile([P, 2, IMAGE], F32, tag="summed")
+                for s in range(2):
+                    j = 2 * pair + s
+                    for t in range(IMAGE_TILES):
+                        nc.tensor.transpose(turned[:, s, t * P : (t + 1) * P], normed[t][:, j * P : (j + 1) * P], ident_f32[:])
+                for s in range(2):
+                    j = 2 * pair + s
+                    nc.vector.scalar_tensor_tensor(
+                        out=summed[:, s, :],
+                        in0=turned[:, s, :],
+                        scalar=ln_cols[:, j : j + 1],
+                        in1=x_shifted[:, j, b, :],
+                        op0=ALU.mult,
+                        op1=ALU.add,
+                    )
+                result = tail.tile([P, 2, IMAGE], F32, tag="result")
+                nc.scalar.activation(out=result[:], in_=summed[:], func=ACT.Relu)
+                nc.sync.dma_start(out=out_view[:, 2 * pair : 2 * pair + 2, :], in_=result[:])
+
+        turn(0)
+        for i in range(1, ROUNDS):
+            turn(i)
+            multiply(i - 1)
+        multiply(ROUNDS - 1)
+        for b in range(BATCH):
+            finish(b)

@@ -15,10 +15,11 @@ ACT = mybir.ActivationFunctionType
 P = 128
 PACK = 4
 K_PASS = P * PACK
+HALVES = 2
+GROUP_WORDS = K_PASS // 2
 BATCH = 2
 IMAGE = 256
 IMAGE_TILES = IMAGE // P
-PIXEL_TILES = BATCH * IMAGE_TILES
 CHANNELS = 512
 CHANNEL_TILES = CHANNELS // P
 K = 16384
@@ -26,7 +27,8 @@ CHUNK_GROUPS = 4
 K_CHUNK = CHUNK_GROUPS * K_PASS
 CHUNKS = K // K_CHUNK
 ROUNDS = CHUNKS * BATCH
-HALVES = 2
+QUADRANTS = 4
+QUADRANT_SCALES = 4
 EPS = 1e-5
 
 H_BUFS = 10
@@ -37,6 +39,10 @@ NORM_SCALE_COL = 16
 SCALAR_COLS = 32
 
 FLOPS = 2 * BATCH * IMAGE * K * CHANNELS
+
+
+def pieces_of_round(i):
+    return CHUNK_GROUPS if i in (0, ROUNDS - 1) else 1
 
 
 def tile_transformerconvblock_pc_k_kernel(
@@ -52,9 +58,23 @@ def tile_transformerconvblock_pc_k_kernel(
         h_pool = ctx.enter_context(tc.tile_pool(name="h_pool", bufs=H_BUFS))
         w_pool = ctx.enter_context(tc.tile_pool(name="w_pool", bufs=W_BUFS))
         work = ctx.enter_context(tc.tile_pool(name="work", bufs=2))
-        tail = ctx.enter_context(tc.tile_pool(name="tail", bufs=2))
+        tail = ctx.enter_context(tc.tile_pool(name="tail", bufs=BATCH * IMAGE_TILES))
         acc_pool = ctx.enter_context(tc.psum_pool(name="acc_pool", bufs=1))
         turn_pool = ctx.enter_context(tc.psum_pool(name="turn_pool", bufs=4))
+
+        one_row = consts.tile([P, CHANNELS + SCALAR_COLS], BF16)
+        nc.vector.memset(one_row[:], 0.0)
+        ln_rows = consts.tile([P, P], BF16)
+        nc.vector.memset(ln_rows[:], 0.0)
+        ffn_col = CHANNELS + FFN_SCALE_COL
+        norm_col = CHANNELS + NORM_SCALE_COL
+        nc.scalar.dma_start(out=one_row[0:1, 0:CHANNELS], in_=ffn2_b.unsqueeze(0))
+        nc.scalar.dma_start(out=one_row[0:1, ffn_col : ffn_col + 1], in_=scale_ffn.unsqueeze(0))
+        nc.scalar.dma_start(out=one_row[0:1, norm_col : norm_col + 1], in_=scale_norm2.unsqueeze(0))
+        nc.scalar.dma_start(out=ln_rows[0:CHANNEL_TILES, :], in_=ln2_w.rearrange("(j c) -> j c", c=P))
+        nc.scalar.dma_start(
+            out=ln_rows[CHANNEL_TILES : 2 * CHANNEL_TILES, :], in_=ln2_b.rearrange("(j c) -> j c", c=P)
+        )
 
         h_tiles = {}
         w_tiles = {}
@@ -62,45 +82,38 @@ def tile_transformerconvblock_pc_k_kernel(
         def load_h(i):
             chunk, b = divmod(i, BATCH)
             h_rows = h_pool.tile([P, IMAGE_TILES, K_CHUNK], BF16, tag="h_rows")
-            nc.sync.dma_start(
-                out=h_rows[:],
-                in_=h_view[:, b * IMAGE_TILES : (b + 1) * IMAGE_TILES, chunk * K_CHUNK : (chunk + 1) * K_CHUNK],
-            )
+            piece_k = K_CHUNK // pieces_of_round(i)
+            for piece in range(pieces_of_round(i)):
+                nc.sync.dma_start(
+                    out=h_rows[:, :, piece * piece_k : (piece + 1) * piece_k],
+                    in_=h_view[
+                        :,
+                        b * IMAGE_TILES : (b + 1) * IMAGE_TILES,
+                        chunk * K_CHUNK + piece * piece_k : chunk * K_CHUNK + (piece + 1) * piece_k,
+                    ],
+                )
             h_tiles[i] = h_rows
-
-        def load_w(chunk):
-            w_words = w_pool.tile([P, CHUNK_GROUPS, PACK * CHANNELS], U8, tag="w_words", align_bytes=64)
-            nc.sync.dma_start(
-                out=w_words[:].bitcast(I32),
-                in_=w_view[:, chunk * CHUNK_GROUPS : (chunk + 1) * CHUNK_GROUPS, :].bitcast(I32),
-            )
-            w_tiles[chunk] = w_words
 
         w_planes = consts.tile([P, CHUNKS, CHANNELS], U8, align_bytes=64)
         nc.vector.memset(w_planes[:].bitcast(I32), 0)
 
-        def load_w_planes():
-            for quadrant in range(4):
-                for r in range(4):
-                    first = 32 * quadrant + r
-                    nc.sync.dma_start(
-                        out=w_planes[first : first + 4 * CHUNK_GROUPS : 4, :, :].bitcast(I32),
-                        in_=ffn2_w_scales[:, 4 * quadrant + r, :]
-                        .rearrange("(a j) n -> j a n", j=CHUNK_GROUPS)
-                        .bitcast(I32),
-                    )
+        def load_w(chunk):
+            groups = slice(chunk * CHUNK_GROUPS, (chunk + 1) * CHUNK_GROUPS)
+            for quadrant in range(QUADRANTS):
+                first = 32 * quadrant
+                rows = slice(quadrant * QUADRANT_SCALES, (quadrant + 1) * QUADRANT_SCALES)
+                nc.sync.dma_start(
+                    out=w_planes[first : first + CHUNK_GROUPS * QUADRANT_SCALES, chunk, :].bitcast(I32),
+                    in_=ffn2_w_scales[groups, rows, :].bitcast(I32),
+                )
+            w_words = w_pool.tile([P, CHUNK_GROUPS, PACK * CHANNELS], U8, tag="w_words", align_bytes=64)
+            nc.sync.dma_start(out=w_words[:].bitcast(I32), in_=w_view[:, groups, :].bitcast(I32))
+            w_tiles[chunk] = w_words
 
-        load_h(0)
-        load_w(0)
-        load_w_planes()
-        for i in range(1, H_BUFS):
+        for i in range(H_BUFS):
             load_h(i)
             if i % BATCH == 0:
                 load_w(i // BATCH)
-
-        x_rows = consts.tile([P, CHANNEL_TILES, BATCH, IMAGE], BF16)
-        for b in range(BATCH):
-            nc.sync.dma_start(out=x_rows[:, :, b, :], in_=x[b].rearrange("(j c) i w -> c j (i w)", c=P))
 
         ident_f32 = consts.tile([P, P], F32)
         make_identity(nc, ident_f32[:])
@@ -113,20 +126,6 @@ def tile_transformerconvblock_pc_k_kernel(
         nc.vector.memset(one_col[:], 1.0)
         sqrt_warm = consts.tile([P, 1], F32)
         nc.scalar.activation(out=sqrt_warm[:], in_=one_col[:], func=ACT.Sqrt)
-
-        one_row = consts.tile([P, CHANNELS + SCALAR_COLS], BF16)
-        nc.vector.memset(one_row[:], 0.0)
-        nc.scalar.dma_start(out=one_row[0:1, 0:CHANNELS], in_=ffn2_b.unsqueeze(0))
-        ffn_col = CHANNELS + FFN_SCALE_COL
-        norm_col = CHANNELS + NORM_SCALE_COL
-        nc.scalar.dma_start(out=one_row[0:1, ffn_col : ffn_col + 1], in_=scale_ffn.unsqueeze(0))
-        nc.scalar.dma_start(out=one_row[0:1, norm_col : norm_col + 1], in_=scale_norm2.unsqueeze(0))
-        ln_rows = consts.tile([P, P], BF16)
-        nc.vector.memset(ln_rows[:], 0.0)
-        nc.scalar.dma_start(out=ln_rows[0:CHANNEL_TILES, :], in_=ln2_w.rearrange("(j c) -> j c", c=P))
-        nc.scalar.dma_start(
-            out=ln_rows[CHANNEL_TILES : 2 * CHANNEL_TILES, :], in_=ln2_b.rearrange("(j c) -> j c", c=P)
-        )
 
         bias_bank = turn_pool.tile([P, CHANNELS], F32, tag="turn")
         nc.tensor.matmul(out=bias_bank[:], lhsT=ones[:], rhs=one_row[:, 0:CHANNELS], start=True, stop=True)
@@ -151,28 +150,22 @@ def tile_transformerconvblock_pc_k_kernel(
             out=ln_cols[:], in0=ln_bank[:, 0 : 2 * CHANNEL_TILES], scalar1=norm_scale, scalar2=None, op0=ALU.mult
         )
 
-        x_shifted = consts.tile([P, CHANNEL_TILES, BATCH, IMAGE], F32)
-        for j in range(CHANNEL_TILES):
-            nc.gpsimd.tensor_scalar(
-                out=x_shifted[:, j, :, :],
-                in0=x_rows[:, j, :, :],
-                scalar1=1.0,
-                scalar2=ln_cols[:, CHANNEL_TILES + j : CHANNEL_TILES + j + 1],
-                op0=ALU.mult,
-                op1=ALU.add,
-            )
-
-        acc = [acc_pool.tile([P, CHANNELS], F32, name="acc%d" % t) for t in range(PIXEL_TILES)]
+        acc = [acc_pool.tile([P, CHANNELS], F32, name="acc%d" % t) for t in range(BATCH * IMAGE_TILES)]
 
         grouped_tiles = {}
 
         def turn(i):
             h_words = h_tiles.pop(i)[:].bitcast(F32)
             sorted_words = work.tile([P, IMAGE_TILES, CHUNK_GROUPS, HALVES, P], F32, tag="sorted_words")
-            nc.vector.tensor_copy(
-                out=sorted_words[:],
-                in_=h_words.rearrange("p t (g q u) -> p t g u q", g=CHUNK_GROUPS, u=HALVES),
-            )
+            piece_groups = CHUNK_GROUPS // pieces_of_round(i)
+            for piece in range(pieces_of_round(i)):
+                groups = slice(piece * piece_groups, (piece + 1) * piece_groups)
+                nc.vector.tensor_copy(
+                    out=sorted_words[:, :, groups, :, :],
+                    in_=h_words[
+                        :, :, piece * piece_groups * GROUP_WORDS : (piece + 1) * piece_groups * GROUP_WORDS
+                    ].rearrange("p t (g q u) -> p t g u q", g=piece_groups, u=HALVES),
+                )
             if i + H_BUFS < ROUNDS:
                 load_h(i + H_BUFS)
             grouped = work.tile([P, CHUNK_GROUPS, IMAGE * PACK], BF16, tag="grouped", align_bytes=64)
@@ -203,61 +196,101 @@ def tile_transformerconvblock_pc_k_kernel(
                         lhsT=h_codes[:, g, pixels].bitcast(FP8X4),
                         lhsT_scale=h_planes[:, g, pixels],
                         rhs=w_words[:, g, :].bitcast(FP8X4),
-                        rhs_scale=w_planes[4 * g : P, chunk, :],
+                        rhs_scale=w_planes[QUADRANT_SCALES * g : P, chunk, :],
                         start=(chunk == 0 and g == 0),
                         stop=(chunk == CHUNKS - 1 and g == CHUNK_GROUPS - 1),
                     )
             if b == BATCH - 1 and chunk + W_BUFS < CHUNKS:
                 load_w(chunk + W_BUFS)
 
-        def finish(b):
-            normed = []
+        biased_tiles = {}
+        mean_var_tiles = {}
+        spread_tiles = {}
+        unit_tiles = {}
+
+        def add_bias(b):
             for t in range(IMAGE_TILES):
                 biased = tail.tile([P, CHANNELS], F32, tag="biased")
                 nc.vector.tensor_tensor(out=biased[:], in0=acc[b * IMAGE_TILES + t][:], in1=bias_all[:], op=ALU.add)
+                biased_tiles[b, t] = biased
+
+        def statistics(b):
+            mean_var = tail.tile([P, IMAGE_TILES, 2], F32, tag="mean_var")
+            for t in range(IMAGE_TILES):
                 stats = tail.tile([P, 6], F32, tag="stats")
-                nc.vector.bn_stats(out=stats[:], in_=biased[:])
-                mean_var = tail.tile([P, 2], F32, tag="mean_var")
-                nc.vector.bn_aggr(out=mean_var[:], in_=stats[:])
-                spread = tail.tile([P, 1], F32, tag="spread")
-                nc.vector.tensor_scalar(
-                    out=spread[:], in0=mean_var[:, 1:2], scalar1=ffn_scale_sq[:], scalar2=EPS, op0=ALU.mult, op1=ALU.add
-                )
-                nc.scalar.activation(out=spread[:], in_=spread[:], func=ACT.Sqrt)
-                gain = tail.tile([P, 1], F32, tag="gain")
-                nc.vector.reciprocal(out=gain[:], in_=spread[:])
-                nc.vector.tensor_scalar(out=gain[:], in0=gain[:], scalar1=ffn_scale, scalar2=None, op0=ALU.mult)
+                nc.vector.bn_stats(out=stats[:], in_=biased_tiles[b, t][:])
+                nc.vector.bn_aggr(out=mean_var[:, t, :], in_=stats[:])
+            spread = tail.tile([P, IMAGE_TILES], F32, tag="spread")
+            nc.vector.tensor_scalar(
+                out=spread[:], in0=mean_var[:, :, 1], scalar1=ffn_scale_sq[:], scalar2=EPS, op0=ALU.mult, op1=ALU.add
+            )
+            nc.scalar.activation(out=spread[:], in_=spread[:], func=ACT.Sqrt)
+            mean_var_tiles[b] = mean_var
+            spread_tiles[b] = spread
+
+        def normalise(b):
+            gain = tail.tile([P, IMAGE_TILES], F32, tag="gain")
+            nc.vector.reciprocal(out=gain[:], in_=spread_tiles[b][:])
+            nc.vector.tensor_scalar(out=gain[:], in0=gain[:], scalar1=ffn_scale, scalar2=None, op0=ALU.mult)
+            for t in range(IMAGE_TILES):
                 unit = tail.tile([P, CHANNELS], F32, tag="unit")
                 nc.vector.tensor_scalar(
-                    out=unit[:], in0=biased[:], scalar1=mean_var[:, 0:1], scalar2=gain[:], op0=ALU.subtract, op1=ALU.mult
+                    out=unit[:],
+                    in0=biased_tiles[b, t][:],
+                    scalar1=mean_var_tiles[b][:, t, 0:1],
+                    scalar2=gain[:, t : t + 1],
+                    op0=ALU.subtract,
+                    op1=ALU.mult,
                 )
-                normed.append(unit)
+                unit_tiles[b, t] = unit
+
+        def write_out(b):
             out_view = out[b].rearrange("(j c) i w -> c j (i w)", c=P)
             for pair in range(CHANNEL_TILES // 2):
                 turned = turn_pool.tile([P, 2, IMAGE], F32, tag="turn")
-                summed = tail.tile([P, 2, IMAGE], F32, tag="summed")
                 for s in range(2):
                     j = 2 * pair + s
                     for t in range(IMAGE_TILES):
-                        nc.tensor.transpose(turned[:, s, t * P : (t + 1) * P], normed[t][:, j * P : (j + 1) * P], ident_f32[:])
+                        nc.tensor.transpose(
+                            turned[:, s, t * P : (t + 1) * P], unit_tiles[b, t][:, j * P : (j + 1) * P], ident_f32[:]
+                        )
+                summed = tail.tile([P, 2, IMAGE], F32, tag="summed")
+                result = tail.tile([P, 2, IMAGE], F32, tag="result")
                 for s in range(2):
                     j = 2 * pair + s
                     nc.vector.scalar_tensor_tensor(
                         out=summed[:, s, :],
                         in0=turned[:, s, :],
                         scalar=ln_cols[:, j : j + 1],
-                        in1=x_shifted[:, j, b, :],
+                        in1=x_rows[:, j, b, :],
                         op0=ALU.mult,
                         op1=ALU.add,
                     )
-                result = tail.tile([P, 2, IMAGE], F32, tag="result")
-                nc.scalar.activation(out=result[:], in_=summed[:], func=ACT.Relu)
+                    nc.scalar.activation(
+                        out=result[:, s, :],
+                        in_=summed[:, s, :],
+                        func=ACT.Relu,
+                        bias=ln_cols[:, CHANNEL_TILES + j : CHANNEL_TILES + j + 1],
+                    )
                 nc.sync.dma_start(out=out_view[:, 2 * pair : 2 * pair + 2, :], in_=result[:])
 
         turn(0)
-        for i in range(1, ROUNDS):
+        for i in range(1, ROUNDS - 1):
             turn(i)
             multiply(i - 1)
-        multiply(ROUNDS - 1)
+        multiply(ROUNDS - 2)
+
+        x_rows = consts.tile([P, CHANNEL_TILES, BATCH, IMAGE], BF16)
         for b in range(BATCH):
-            finish(b)
+            nc.sync.dma_start(out=x_rows[:, :, b, :], in_=x[b].rearrange("(j c) i w -> c j (i w)", c=P))
+
+        turn(ROUNDS - 1)
+        add_bias(0)
+        multiply(ROUNDS - 1)
+        statistics(0)
+        add_bias(1)
+        statistics(1)
+        for b in range(BATCH):
+            normalise(b)
+        for b in range(BATCH):
+            write_out(b)

@@ -112,7 +112,7 @@ def tile_transformerconvblock_pc_k_kernel(
 
         for i in range(H_BUFS):
             load_h(i)
-            if i % BATCH == 0:
+            if i % BATCH == BATCH - 1:
                 load_w(i // BATCH)
 
         ident_f32 = consts.tile([P, P], F32)

@@ -59,6 +59,7 @@ def tile_transformerconvblock_pc_k_kernel(
         w_pool = ctx.enter_context(tc.tile_pool(name="w_pool", bufs=W_BUFS))
         work = ctx.enter_context(tc.tile_pool(name="work", bufs=2))
         tail = ctx.enter_context(tc.tile_pool(name="tail", bufs=BATCH * IMAGE_TILES))
+        out_pool = ctx.enter_context(tc.tile_pool(name="out_pool", bufs=BATCH * CHANNEL_TILES))
         acc_pool = ctx.enter_context(tc.psum_pool(name="acc_pool", bufs=1))
         turn_pool = ctx.enter_context(tc.psum_pool(name="turn_pool", bufs=4))
 
@@ -149,6 +150,9 @@ def tile_transformerconvblock_pc_k_kernel(
         nc.vector.tensor_scalar(
             out=ln_cols[:], in0=ln_bank[:, 0 : 2 * CHANNEL_TILES], scalar1=norm_scale, scalar2=None, op0=ALU.mult
         )
+        nc.vector.tensor_scalar(
+            out=ln_cols[:, 0:CHANNEL_TILES], in0=ln_cols[:, 0:CHANNEL_TILES], scalar1=ffn_scale, scalar2=None, op0=ALU.mult
+        )
 
         acc = [acc_pool.tile([P, CHANNELS], F32, name="acc%d" % t) for t in range(BATCH * IMAGE_TILES)]
 
@@ -231,7 +235,6 @@ def tile_transformerconvblock_pc_k_kernel(
         def normalise(b):
             gain = tail.tile([P, IMAGE_TILES], F32, tag="gain")
             nc.vector.reciprocal(out=gain[:], in_=spread_tiles[b][:])
-            nc.vector.tensor_scalar(out=gain[:], in0=gain[:], scalar1=ffn_scale, scalar2=None, op0=ALU.mult)
             for t in range(IMAGE_TILES):
                 unit = tail.tile([P, CHANNELS], F32, tag="unit")
                 nc.vector.tensor_scalar(
@@ -246,33 +249,29 @@ def tile_transformerconvblock_pc_k_kernel(
 
         def write_out(b):
             out_view = out[b].rearrange("(j c) i w -> c j (i w)", c=P)
-            for pair in range(CHANNEL_TILES // 2):
-                turned = turn_pool.tile([P, 2, IMAGE], F32, tag="turn")
-                for s in range(2):
-                    j = 2 * pair + s
-                    for t in range(IMAGE_TILES):
-                        nc.tensor.transpose(
-                            turned[:, s, t * P : (t + 1) * P], unit_tiles[b, t][:, j * P : (j + 1) * P], ident_f32[:]
-                        )
-                summed = tail.tile([P, 2, IMAGE], F32, tag="summed")
-                result = tail.tile([P, 2, IMAGE], F32, tag="result")
-                for s in range(2):
-                    j = 2 * pair + s
-                    nc.vector.scalar_tensor_tensor(
-                        out=summed[:, s, :],
-                        in0=turned[:, s, :],
-                        scalar=ln_cols[:, j : j + 1],
-                        in1=x_rows[:, j, b, :],
-                        op0=ALU.mult,
-                        op1=ALU.add,
+            for j in range(CHANNEL_TILES):
+                turned = turn_pool.tile([P, IMAGE], F32, tag="turn")
+                for t in range(IMAGE_TILES):
+                    nc.tensor.transpose(
+                        turned[:, t * P : (t + 1) * P], unit_tiles[b, t][:, j * P : (j + 1) * P], ident_f32[:]
                     )
-                    nc.scalar.activation(
-                        out=result[:, s, :],
-                        in_=summed[:, s, :],
-                        func=ACT.Relu,
-                        bias=ln_cols[:, CHANNEL_TILES + j : CHANNEL_TILES + j + 1],
-                    )
-                nc.sync.dma_start(out=out_view[:, 2 * pair : 2 * pair + 2, :], in_=result[:])
+                summed = tail.tile([P, IMAGE], F32, tag="summed")
+                nc.vector.scalar_tensor_tensor(
+                    out=summed[:],
+                    in0=turned[:],
+                    scalar=ln_cols[:, j : j + 1],
+                    in1=x_rows[:, j, b, :],
+                    op0=ALU.mult,
+                    op1=ALU.add,
+                )
+                result = out_pool.tile([P, IMAGE], F32, tag="result")
+                nc.scalar.activation(
+                    out=result[:],
+                    in_=summed[:],
+                    func=ACT.Relu,
+                    bias=ln_cols[:, CHANNEL_TILES + j : CHANNEL_TILES + j + 1],
+                )
+                nc.sync.dma_start(out=out_view[:, j, :], in_=result[:])
 
         turn(0)
         for i in range(1, ROUNDS - 1):

@@ -16,33 +16,62 @@ P = 128
 PACK = 4
 K_PASS = P * PACK
 HALVES = 2
-GROUP_WORDS = K_PASS // 2
 BATCH = 2
 IMAGE = 256
-IMAGE_TILES = IMAGE // P
+IMAGE_TILES = 2
+TILES = 4
 CHANNELS = 512
-CHANNEL_TILES = CHANNELS // P
+CHANNEL_TILES = 4
 K = 16384
+GROUPS = K // K_PASS
 CHUNK_GROUPS = 4
-K_CHUNK = CHUNK_GROUPS * K_PASS
-CHUNKS = K // K_CHUNK
-ROUNDS = CHUNKS * BATCH
+CHUNKS = GROUPS // CHUNK_GROUPS
+BANKS = 4
+SLOTS = 2
+SLAB_K = BANKS * SLOTS * K_PASS
 QUADRANTS = 4
 QUADRANT_SCALES = 4
 EPS = 1e-5
-
-H_BUFS = 10
-W_BUFS = H_BUFS // BATCH
-
 FFN_SCALE_COL = 0
 NORM_SCALE_COL = 16
 SCALAR_COLS = 32
-
 FLOPS = 2 * BATCH * IMAGE * K * CHANNELS
 
+TILE_END_CHUNKS = 0
+TILE_MAJOR = (0,)
+SPLITS = {0: 4}
+W_PIECES = {}
+SCALES_FIRST = False
+MOVES = []
+X_BEFORE = (0, 0)
+CONST_AFTER = 0
+H_BUFS = 10
+W_BUFS = 5
+SORT_BUFS = 2
+STORE_EVERY = 4
+AFTER_TURN = {}
+AFTER_QUANTISE = {}
+AFTER_MULTIPLY = {0: "bias0 bias1 stats0 stats1 bias2 bias3 stats2 stats3 normv0 normv1 normv2 normv3 tout0 fin0 tout1 fin1 tout2 fin2 tout3 fin3"}
 
-def pieces_of_round(i):
-    return CHUNK_GROUPS if i in (0, ROUNDS - 1) else 1
+
+def make_slabs():
+    slabs = []
+    image_chunks = CHUNKS - TILE_END_CHUNKS
+    for chunk in range(image_chunks):
+        for b in range(BATCH):
+            slabs.append(((IMAGE_TILES * b, IMAGE_TILES * b + 1), chunk * CHUNK_GROUPS, CHUNK_GROUPS))
+    if TILE_END_CHUNKS:
+        for t in range(TILES):
+            slabs.append(((t,), image_chunks * CHUNK_GROUPS, TILE_END_CHUNKS * CHUNK_GROUPS))
+    return slabs
+
+
+def units_of_bank(i, slab, j):
+    tiles, first, groups = slab
+    if len(tiles) == SLOTS and i not in TILE_MAJOR:
+        return [(t, first + j) for t in tiles]
+    per_tile = BANKS // len(tiles)
+    return [(tiles[j // per_tile], first + SLOTS * (j % per_tile) + s) for s in range(SLOTS)]
 
 
 def tile_transformerconvblock_pc_k_kernel(
@@ -51,15 +80,23 @@ def tile_transformerconvblock_pc_k_kernel(
     nc = tc.nc
     h_view = h.flatten_outer_dims().rearrange("(t p) k -> p t k", p=P)
     w_view = ffn2_w_words.rearrange("g p n t -> p g (n t)")
+    slabs = make_slabs()
+    items = []
+    for i in range(len(slabs)):
+        parts = SPLITS.get(i, 1)
+        step = BANKS // parts
+        for a in range(parts):
+            items.append((i, a * step, (a + 1) * step))
+    n_items = len(items)
 
     with ExitStack() as ctx:
         ctx.enter_context(tc.manual_schedule())
         consts = ctx.enter_context(tc.tile_pool(name="consts", bufs=1))
         h_pool = ctx.enter_context(tc.tile_pool(name="h_pool", bufs=H_BUFS))
         w_pool = ctx.enter_context(tc.tile_pool(name="w_pool", bufs=W_BUFS))
+        sort_pool = ctx.enter_context(tc.tile_pool(name="sort_pool", bufs=SORT_BUFS))
         work = ctx.enter_context(tc.tile_pool(name="work", bufs=2))
-        tail = ctx.enter_context(tc.tile_pool(name="tail", bufs=BATCH * IMAGE_TILES))
-        out_pool = ctx.enter_context(tc.tile_pool(name="out_pool", bufs=BATCH * CHANNEL_TILES))
+        tail = ctx.enter_context(tc.tile_pool(name="tail", bufs=TILES))
         acc_pool = ctx.enter_context(tc.psum_pool(name="acc_pool", bufs=1))
         turn_pool = ctx.enter_context(tc.psum_pool(name="turn_pool", bufs=4))
 
@@ -77,44 +114,112 @@ def tile_transformerconvblock_pc_k_kernel(
             out=ln_rows[CHANNEL_TILES : 2 * CHANNEL_TILES, :], in_=ln2_b.rearrange("(j c) -> j c", c=P)
         )
 
-        h_tiles = {}
-        w_tiles = {}
-
-        def load_h(i):
-            chunk, b = divmod(i, BATCH)
-            h_rows = h_pool.tile([P, IMAGE_TILES, K_CHUNK], BF16, tag="h_rows")
-            piece_k = K_CHUNK // pieces_of_round(i)
-            for piece in range(pieces_of_round(i)):
-                nc.sync.dma_start(
-                    out=h_rows[:, :, piece * piece_k : (piece + 1) * piece_k],
-                    in_=h_view[
-                        :,
-                        b * IMAGE_TILES : (b + 1) * IMAGE_TILES,
-                        chunk * K_CHUNK + piece * piece_k : chunk * K_CHUNK + (piece + 1) * piece_k,
-                    ],
-                )
-            h_tiles[i] = h_rows
-
         w_planes = consts.tile([P, CHUNKS, CHANNELS], U8, align_bytes=64)
         nc.vector.memset(w_planes[:].bitcast(I32), 0)
+        x_rows = consts.tile([P, CHANNEL_TILES, BATCH, IMAGE], BF16)
 
-        def load_w(chunk):
-            groups = slice(chunk * CHUNK_GROUPS, (chunk + 1) * CHUNK_GROUPS)
-            for quadrant in range(QUADRANTS):
-                first = 32 * quadrant
-                rows = slice(quadrant * QUADRANT_SCALES, (quadrant + 1) * QUADRANT_SCALES)
+        plan = []
+        planned = set()
+        last_use = {}
+        for k in range(n_items + 1):
+            if k < n_items:
+                plan.append(("h",) + items[k])
+            if k >= 1:
+                i, j0, j1 = items[k - 1]
+                for j in range(j0, j1):
+                    for t, g in units_of_bank(i, slabs[i], j):
+                        chunk = g // CHUNK_GROUPS
+                        last_use[chunk] = k - 1
+                        pieces = W_PIECES.get(chunk, 1)
+                        piece = (g % CHUNK_GROUPS) * pieces // CHUNK_GROUPS
+                        if ("s", chunk) not in planned and not SCALES_FIRST:
+                            planned.add(("s", chunk))
+                            plan.append(("s", chunk))
+                        if ("w", chunk, piece) not in planned:
+                            planned.add(("w", chunk, piece))
+                            plan.append(("w", chunk, piece))
+        if SCALES_FIRST:
+            where = [n for n, e in enumerate(plan) if e[0] == "w"][0]
+            plan[where:where] = [("s", chunk) for chunk in range(CHUNKS)]
+        for chunk, slab in MOVES:
+            moved = [e for e in plan if e[0] in ("s", "w") and e[1] == chunk]
+            plan = [e for e in plan if e not in moved]
+            where = [n for n, e in enumerate(plan) if e[0] == "h" and e[1] == slab][0]
+            plan[where:where] = moved
+        h_places = [n for n, e in enumerate(plan) if e[0] == "h"]
+        for b in reversed(range(BATCH)):
+            back = X_BEFORE[b]
+            if back:
+                plan[h_places[-back] : h_places[-back]] = [("x", b)]
+            else:
+                plan.append(("x", b))
+
+        h_tiles = {}
+        w_tiles = {}
+        state = {"next": 0, "sorted": 0, "chunks": 0}
+
+        def issue(entry):
+            kind = entry[0]
+            if kind == "h":
+                i, j0, j1 = entry[1:]
+                tiles, first, groups = slabs[i]
+                if i not in h_tiles:
+                    h_rows = h_pool.tile([P, SLAB_K], BF16, tag="h_rows")
+                    h_tiles[i] = h_rows
+                by_tile = h_tiles[i][:].rearrange("p (t k) -> p t k", t=len(tiles))
+                width = SLAB_K // len(tiles)
+                if len(tiles) == SLOTS and i not in TILE_MAJOR:
+                    per_bank = width // BANKS
+                    spans = [(0, len(tiles), j0 * per_bank, j1 * per_bank)]
+                elif j1 - j0 == BANKS:
+                    spans = [(0, len(tiles), 0, width)]
+                else:
+                    per_tile = BANKS // len(tiles)
+                    per_bank = width // per_tile
+                    assert j0 // per_tile == (j1 - 1) // per_tile
+                    spans = [(j0 // per_tile, j0 // per_tile + 1, (j0 % per_tile) * per_bank, (j0 % per_tile + j1 - j0) * per_bank)]
+                for t0, t1, k0, k1 in spans:
+                    nc.sync.dma_start(
+                        out=by_tile[:, t0:t1, k0:k1],
+                        in_=h_view[:, tiles[0] + t0 : tiles[0] + t1, first * K_PASS + k0 : first * K_PASS + k1],
+                    )
+            elif kind == "s":
+                chunk = entry[1]
+                groups = slice(chunk * CHUNK_GROUPS, (chunk + 1) * CHUNK_GROUPS)
+                for quadrant in range(QUADRANTS):
+                    first = 32 * quadrant
+                    rows = slice(quadrant * QUADRANT_SCALES, (quadrant + 1) * QUADRANT_SCALES)
+                    nc.sync.dma_start(
+                        out=w_planes[first : first + CHUNK_GROUPS * QUADRANT_SCALES, chunk, :].bitcast(I32),
+                        in_=ffn2_w_scales[groups, rows, :].bitcast(I32),
+                    )
+            elif kind == "w":
+                chunk, piece = entry[1:]
+                if chunk not in w_tiles:
+                    w_words = w_pool.tile([P, CHUNK_GROUPS, PACK * CHANNELS], U8, tag="w_words", align_bytes=64)
+                    w_tiles[chunk] = w_words
+                per = CHUNK_GROUPS // W_PIECES.get(chunk, 1)
                 nc.sync.dma_start(
-                    out=w_planes[first : first + CHUNK_GROUPS * QUADRANT_SCALES, chunk, :].bitcast(I32),
-                    in_=ffn2_w_scales[groups, rows, :].bitcast(I32),
+                    out=w_tiles[chunk][:, piece * per : (piece + 1) * per, :].bitcast(I32),
+                    in_=w_view[
+                        :, chunk * CHUNK_GROUPS + piece * per : chunk * CHUNK_GROUPS + (piece + 1) * per, :
+                    ].bitcast(I32),
                 )
-            w_words = w_pool.tile([P, CHUNK_GROUPS, PACK * CHANNELS], U8, tag="w_words", align_bytes=64)
-            nc.sync.dma_start(out=w_words[:].bitcast(I32), in_=w_view[:, groups, :].bitcast(I32))
-            w_tiles[chunk] = w_words
+            else:
+                b = entry[1]
+                nc.sync.dma_start(out=x_rows[:, :, b, :], in_=x[b].rearrange("(j c) i w -> c j (i w)", c=P))
 
-        for i in range(H_BUFS):
-            load_h(i)
-            if i % BATCH == BATCH - 1:
-                load_w(i // BATCH)
+        def pump():
+            while state["next"] < len(plan):
+                entry = plan[state["next"]]
+                if entry[0] == "h" and entry[1] >= H_BUFS + state["sorted"]:
+                    return
+                if entry[0] == "w" and entry[1] >= W_BUFS + state["chunks"]:
+                    return
+                issue(entry)
+                state["next"] += 1
+
+        pump()
 
         ident_f32 = consts.tile([P, P], F32)
         make_identity(nc, ident_f32[:])
@@ -122,174 +227,220 @@ def tile_transformerconvblock_pc_k_kernel(
         make_identity(nc, ident_bf16[:])
         ones = consts.tile([P, P], BF16)
         nc.vector.memset(ones[:], 1.0)
-
         one_col = consts.tile([P, 1], F32)
         nc.vector.memset(one_col[:], 1.0)
         sqrt_warm = consts.tile([P, 1], F32)
         nc.scalar.activation(out=sqrt_warm[:], in_=one_col[:], func=ACT.Sqrt)
 
-        bias_bank = turn_pool.tile([P, CHANNELS], F32, tag="turn")
-        nc.tensor.matmul(out=bias_bank[:], lhsT=ones[:], rhs=one_row[:, 0:CHANNELS], start=True, stop=True)
         bias_all = consts.tile([P, CHANNELS], F32)
-        nc.vector.tensor_copy(out=bias_all[:], in_=bias_bank[:])
-
-        scalar_bank = turn_pool.tile([P, SCALAR_COLS], F32, tag="turn")
-        nc.tensor.matmul(
-            out=scalar_bank[:], lhsT=ones[:], rhs=one_row[:, CHANNELS : CHANNELS + SCALAR_COLS], start=True, stop=True
-        )
         scalars = consts.tile([P, SCALAR_COLS], F32)
-        nc.vector.tensor_copy(out=scalars[:], in_=scalar_bank[:])
         ffn_scale = scalars[:, FFN_SCALE_COL : FFN_SCALE_COL + 1]
         norm_scale = scalars[:, NORM_SCALE_COL : NORM_SCALE_COL + 1]
         ffn_scale_sq = consts.tile([P, 1], F32)
-        nc.vector.tensor_tensor(out=ffn_scale_sq[:], in0=ffn_scale, in1=ffn_scale, op=ALU.mult)
-
-        ln_bank = turn_pool.tile([P, P], BF16, tag="turn")
-        nc.tensor.transpose(ln_bank[:], ln_rows[:], ident_bf16[:])
         ln_cols = consts.tile([P, 2 * CHANNEL_TILES], F32)
-        nc.vector.tensor_scalar(
-            out=ln_cols[:], in0=ln_bank[:, 0 : 2 * CHANNEL_TILES], scalar1=norm_scale, scalar2=None, op0=ALU.mult
-        )
-        nc.vector.tensor_scalar(
-            out=ln_cols[:, 0:CHANNEL_TILES], in0=ln_cols[:, 0:CHANNEL_TILES], scalar1=ffn_scale, scalar2=None, op0=ALU.mult
-        )
 
-        acc = [acc_pool.tile([P, CHANNELS], F32, name="acc%d" % t) for t in range(BATCH * IMAGE_TILES)]
+        def make_constants():
+            bias_bank = turn_pool.tile([P, CHANNELS], F32, tag="turn")
+            nc.tensor.matmul(out=bias_bank[:], lhsT=ones[:], rhs=one_row[:, 0:CHANNELS], start=True, stop=True)
+            nc.scalar.copy(out=bias_all[:], in_=bias_bank[:])
+            scalar_bank = turn_pool.tile([P, SCALAR_COLS], F32, tag="turn")
+            nc.tensor.matmul(
+                out=scalar_bank[:], lhsT=ones[:], rhs=one_row[:, CHANNELS : CHANNELS + SCALAR_COLS], start=True, stop=True
+            )
+            nc.scalar.copy(out=scalars[:], in_=scalar_bank[:])
+            nc.scalar.activation(out=ffn_scale_sq[:], in_=ffn_scale, func=ACT.Copy, scale=ffn_scale)
+            ln_bank = turn_pool.tile([P, P], BF16, tag="turn")
+            nc.tensor.transpose(ln_bank[:], ln_rows[:], ident_bf16[:])
+            nc.scalar.activation(out=ln_cols[:], in_=ln_bank[:, 0 : 2 * CHANNEL_TILES], func=ACT.Copy, scale=norm_scale)
+            nc.scalar.activation(
+                out=ln_cols[:, 0:CHANNEL_TILES], in_=ln_cols[:, 0:CHANNEL_TILES], func=ACT.Copy, scale=ffn_scale
+            )
 
+        acc = [acc_pool.tile([P, CHANNELS], F32, name="acc%d" % t) for t in range(TILES)]
+
+        sorted_tiles = {}
         grouped_tiles = {}
+        code_tiles = {}
 
-        def turn(i):
-            h_words = h_tiles.pop(i)[:].bitcast(F32)
-            sorted_words = work.tile([P, IMAGE_TILES, CHUNK_GROUPS, HALVES, P], F32, tag="sorted_words")
-            piece_groups = CHUNK_GROUPS // pieces_of_round(i)
-            for piece in range(pieces_of_round(i)):
-                groups = slice(piece * piece_groups, (piece + 1) * piece_groups)
-                nc.vector.tensor_copy(
-                    out=sorted_words[:, :, groups, :, :],
-                    in_=h_words[
-                        :, :, piece * piece_groups * GROUP_WORDS : (piece + 1) * piece_groups * GROUP_WORDS
-                    ].rearrange("p t (g q u) -> p t g u q", g=piece_groups, u=HALVES),
+        def sort(k):
+            i, j0, j1 = items[k]
+            tiles = slabs[i][0]
+            if i not in sorted_tiles:
+                sorted_words = sort_pool.tile([P, BANKS, SLOTS, HALVES, P], F32, tag="sorted_words")
+                sorted_tiles[i] = sorted_words
+            h_words = h_tiles[i][:].bitcast(F32)
+            if len(tiles) == SLOTS and i not in TILE_MAJOR:
+                per_bank = SLAB_K // SLOTS // BANKS // 2
+                source = h_words.rearrange("p (s w) -> p s w", s=SLOTS)[:, :, j0 * per_bank : j1 * per_bank].rearrange(
+                    "p s (j q u) -> p j s u q", j=j1 - j0, u=HALVES
                 )
-            if i + H_BUFS < ROUNDS:
-                load_h(i + H_BUFS)
-            grouped = work.tile([P, CHUNK_GROUPS, IMAGE * PACK], BF16, tag="grouped", align_bytes=64)
-            grouped_words = grouped[:].bitcast(F32).rearrange("p g (x u) -> p g x u", u=HALVES)
-            for g in range(CHUNK_GROUPS):
+            else:
+                per_bank = SLAB_K // BANKS // 2
+                source = h_words[:, j0 * per_bank : j1 * per_bank].rearrange(
+                    "p (j s q u) -> p j s u q", j=j1 - j0, s=SLOTS, u=HALVES
+                )
+            nc.vector.tensor_copy(out=sorted_tiles[i][:, j0:j1, :, :, :], in_=source)
+            if j1 == BANKS:
+                h_tiles.pop(i)
+                state["sorted"] += 1
+                pump()
+
+        def turn(k):
+            i, j0, j1 = items[k]
+            if i not in grouped_tiles:
+                grouped = work.tile([P, BANKS, IMAGE * PACK], BF16, tag="grouped", align_bytes=64)
+                grouped_tiles[i] = grouped
+            grouped_words = grouped_tiles[i][:].bitcast(F32).rearrange("p j (x u) -> p j x u", u=HALVES)
+            for j in range(j0, j1):
                 turned = turn_pool.tile([P, HALVES, IMAGE], F32, tag="turn")
-                for t in range(IMAGE_TILES):
+                for s in range(SLOTS):
                     for u in range(HALVES):
-                        nc.tensor.transpose(turned[:, u, t * P : (t + 1) * P], sorted_words[:, t, g, u, :], ident_f32[:])
-                nc.scalar.copy(out=grouped_words[:, g, :, :], in_=turned[:].rearrange("p u x -> p x u"))
-            grouped_tiles[i] = grouped
+                        nc.tensor.transpose(turned[:, u, s * P : (s + 1) * P], sorted_tiles[i][:, j, s, u, :], ident_f32[:])
+                nc.scalar.copy(out=grouped_words[:, j, :, :], in_=turned[:].rearrange("p u x -> p x u"))
+            if j1 == BANKS:
+                sorted_tiles.pop(i)
 
-        def multiply(i):
-            chunk, b = divmod(i, BATCH)
-            grouped = grouped_tiles.pop(i)
-            h_codes = work.tile([P, CHUNK_GROUPS, IMAGE], U32, tag="h_codes", align_bytes=64)
-            h_planes = work.tile([P, CHUNK_GROUPS, IMAGE], U8, tag="h_planes", align_bytes=64)
-            for g in range(CHUNK_GROUPS):
+        def quantise(k):
+            i, j0, j1 = items[k]
+            if i not in code_tiles:
+                h_codes = work.tile([P, BANKS, IMAGE], U32, tag="h_codes", align_bytes=64)
+                h_planes = work.tile([P, BANKS, IMAGE], U8, tag="h_planes", align_bytes=64)
+                code_tiles[i] = (h_codes, h_planes)
+            h_codes, h_planes = code_tiles[i]
+            for j in range(j0, j1):
                 nc.vector.quantize_mx(
-                    out=h_codes[:, g, :].bitcast(FP8X4), scales=h_planes[:, g, :], in_=grouped[:, g, :]
+                    out=h_codes[:, j, :].bitcast(FP8X4), scales=h_planes[:, j, :], in_=grouped_tiles[i][:, j, :]
                 )
-            w_words = w_tiles[chunk]
-            for g in range(CHUNK_GROUPS):
-                for t in range(IMAGE_TILES):
-                    pixels = slice(t * P, (t + 1) * P)
+            if j1 == BANKS:
+                grouped_tiles.pop(i)
+
+        def multiply(k):
+            i, j0, j1 = items[k]
+            h_codes, h_planes = code_tiles[i]
+            for j in range(j0, j1):
+                for s, (t, g) in enumerate(units_of_bank(i, slabs[i], j)):
+                    chunk, member = divmod(g, CHUNK_GROUPS)
+                    pixels = slice(s * P, (s + 1) * P)
                     nc.tensor.matmul_mx(
-                        out=acc[b * IMAGE_TILES + t][:],
-                        lhsT=h_codes[:, g, pixels].bitcast(FP8X4),
-                        lhsT_scale=h_planes[:, g, pixels],
-                        rhs=w_words[:, g, :].bitcast(FP8X4),
-                        rhs_scale=w_planes[QUADRANT_SCALES * g : P, chunk, :],
-                        start=(chunk == 0 and g == 0),
-                        stop=(chunk == CHUNKS - 1 and g == CHUNK_GROUPS - 1),
+                        out=acc[t][:],
+                        lhsT=h_codes[:, j, pixels].bitcast(FP8X4),
+                        lhsT_scale=h_planes[:, j, pixels],
+                        rhs=w_tiles[chunk][:, member, :].bitcast(FP8X4),
+                        rhs_scale=w_planes[QUADRANT_SCALES * member : P, chunk, :],
+                        start=(g == 0),
+                        stop=(g == GROUPS - 1),
                     )
-            if b == BATCH - 1 and chunk + W_BUFS < CHUNKS:
-                load_w(chunk + W_BUFS)
+            if j1 == BANKS:
+                code_tiles.pop(i)
+            freed = [chunk for chunk in last_use if last_use[chunk] == k]
+            if freed:
+                state["chunks"] += len(freed)
+                pump()
 
         biased_tiles = {}
         mean_var_tiles = {}
         spread_tiles = {}
+        gain_tiles = {}
         unit_tiles = {}
+        turned_out = {}
 
-        def add_bias(b):
-            for t in range(IMAGE_TILES):
-                biased = tail.tile([P, CHANNELS], F32, tag="biased")
-                nc.vector.tensor_tensor(out=biased[:], in0=acc[b * IMAGE_TILES + t][:], in1=bias_all[:], op=ALU.add)
-                biased_tiles[b, t] = biased
+        def bias(t):
+            biased = tail.tile([P, CHANNELS], F32, tag="biased")
+            nc.vector.tensor_tensor(out=biased[:], in0=acc[t][:], in1=bias_all[:], op=ALU.add)
+            biased_tiles[t] = biased
 
-        def statistics(b):
-            mean_var = tail.tile([P, IMAGE_TILES, 2], F32, tag="mean_var")
-            for t in range(IMAGE_TILES):
-                stats = tail.tile([P, 6], F32, tag="stats")
-                nc.vector.bn_stats(out=stats[:], in_=biased_tiles[b, t][:])
-                nc.vector.bn_aggr(out=mean_var[:, t, :], in_=stats[:])
-            spread = tail.tile([P, IMAGE_TILES], F32, tag="spread")
+        def stats(t):
+            stat = tail.tile([P, 6], F32, tag="stat")
+            nc.vector.bn_stats(out=stat[:], in_=biased_tiles[t][:])
+            mean_var = tail.tile([P, 2], F32, tag="mean_var")
+            nc.vector.bn_aggr(out=mean_var[:], in_=stat[:])
+            spread = tail.tile([P, 1], F32, tag="spread")
             nc.vector.tensor_scalar(
-                out=spread[:], in0=mean_var[:, :, 1], scalar1=ffn_scale_sq[:], scalar2=EPS, op0=ALU.mult, op1=ALU.add
+                out=spread[:], in0=mean_var[:, 1:2], scalar1=ffn_scale_sq[:], scalar2=EPS, op0=ALU.mult, op1=ALU.add
             )
             nc.scalar.activation(out=spread[:], in_=spread[:], func=ACT.Sqrt)
-            mean_var_tiles[b] = mean_var
-            spread_tiles[b] = spread
+            mean_var_tiles[t] = mean_var
+            spread_tiles[t] = spread
 
-        def normalise(b):
-            gain = tail.tile([P, IMAGE_TILES], F32, tag="gain")
-            nc.vector.reciprocal(out=gain[:], in_=spread_tiles[b][:])
-            for t in range(IMAGE_TILES):
-                unit = tail.tile([P, CHANNELS], F32, tag="unit")
-                nc.vector.tensor_scalar(
-                    out=unit[:],
-                    in0=biased_tiles[b, t][:],
-                    scalar1=mean_var_tiles[b][:, t, 0:1],
-                    scalar2=gain[:, t : t + 1],
-                    op0=ALU.subtract,
-                    op1=ALU.mult,
-                )
-                unit_tiles[b, t] = unit
+        def normv(t):
+            gain = tail.tile([P, 1], F32, tag="gain")
+            nc.vector.reciprocal(out=gain[:], in_=spread_tiles[t][:])
+            unit = tail.tile([P, CHANNELS], F32, tag="unit")
+            nc.vector.tensor_scalar(
+                out=unit[:],
+                in0=biased_tiles[t][:],
+                scalar1=mean_var_tiles[t][:, 0:1],
+                scalar2=gain[:],
+                op0=ALU.subtract,
+                op1=ALU.mult,
+            )
+            unit_tiles[t] = unit
 
-        def write_out(b):
-            out_view = out[b].rearrange("(j c) i w -> c j (i w)", c=P)
+        def gain(t):
+            pair = tail.tile([P, 2], F32, tag="pair")
+            nc.vector.reciprocal(out=pair[:, 0:1], in_=spread_tiles[t][:])
+            nc.vector.scalar_tensor_tensor(
+                out=pair[:, 1:2], in0=mean_var_tiles[t][:, 0:1], scalar=-1.0, in1=pair[:, 0:1], op0=ALU.mult, op1=ALU.mult
+            )
+            gain_tiles[t] = pair
+
+        def norms(t):
+            unit = tail.tile([P, CHANNELS], F32, tag="unit")
+            nc.scalar.activation(
+                out=unit[:], in_=biased_tiles[t][:], func=ACT.Identity, scale=gain_tiles[t][:, 0:1], bias=gain_tiles[t][:, 1:2]
+            )
+            unit_tiles[t] = unit
+
+        def tout(t):
+            turned = acc_pool.tile([P, CHANNEL_TILES, P], F32, name="acc%d" % t)
             for j in range(CHANNEL_TILES):
-                turned = turn_pool.tile([P, IMAGE], F32, tag="turn")
-                for t in range(IMAGE_TILES):
-                    nc.tensor.transpose(
-                        turned[:, t * P : (t + 1) * P], unit_tiles[b, t][:, j * P : (j + 1) * P], ident_f32[:]
-                    )
-                summed = tail.tile([P, IMAGE], F32, tag="summed")
+                nc.tensor.transpose(turned[:, j, :], unit_tiles[t][:, j * P : (j + 1) * P], ident_f32[:])
+            turned_out[t] = turned
+
+        def fin(t):
+            b, half = divmod(t, IMAGE_TILES)
+            pixels = slice(half * P, (half + 1) * P)
+            out_view = out[b].rearrange("(j c) i w -> c j (i w)", c=P)
+            summed = tail.tile([P, CHANNEL_TILES, P], F32, tag="summed")
+            result = tail.tile([P, CHANNEL_TILES, P], F32, tag="result")
+            for j in range(CHANNEL_TILES):
                 nc.vector.scalar_tensor_tensor(
-                    out=summed[:],
-                    in0=turned[:],
+                    out=summed[:, j, :],
+                    in0=turned_out[t][:, j, :],
                     scalar=ln_cols[:, j : j + 1],
-                    in1=x_rows[:, j, b, :],
+                    in1=x_rows[:, j, b, pixels],
                     op0=ALU.mult,
                     op1=ALU.add,
                 )
-                result = out_pool.tile([P, IMAGE], F32, tag="result")
                 nc.scalar.activation(
-                    out=result[:],
-                    in_=summed[:],
+                    out=result[:, j, :],
+                    in_=summed[:, j, :],
                     func=ACT.Relu,
                     bias=ln_cols[:, CHANNEL_TILES + j : CHANNEL_TILES + j + 1],
                 )
-                nc.sync.dma_start(out=out_view[:, j, :], in_=result[:])
+                if j % STORE_EVERY == STORE_EVERY - 1:
+                    js = slice(j + 1 - STORE_EVERY, j + 1)
+                    nc.sync.dma_start(out=out_view[:, js, pixels], in_=result[:, js, :])
 
-        turn(0)
-        for i in range(1, ROUNDS - 1):
-            turn(i)
-            multiply(i - 1)
-        multiply(ROUNDS - 2)
+        stages = {"bias": bias, "stats": stats, "normv": normv, "gain": gain, "norms": norms, "tout": tout, "fin": fin}
 
-        x_rows = consts.tile([P, CHANNEL_TILES, BATCH, IMAGE], BF16)
-        for b in range(BATCH):
-            nc.sync.dma_start(out=x_rows[:, :, b, :], in_=x[b].rearrange("(j c) i w -> c j (i w)", c=P))
+        def run(names):
+            for name in names.split():
+                stages[name[:-1]](int(name[-1]))
 
-        turn(ROUNDS - 1)
-        add_bias(0)
-        multiply(ROUNDS - 1)
-        statistics(0)
-        add_bias(1)
-        statistics(1)
-        for b in range(BATCH):
-            normalise(b)
-        for b in range(BATCH):
-            write_out(b)
+        sort(0)
+        for k in range(n_items + 1):
+            back = k - n_items
+            if k < n_items:
+                turn(k)
+            if k == CONST_AFTER:
+                make_constants()
+            run(AFTER_TURN.get(back, ""))
+            if k >= 1:
+                quantise(k - 1)
+            if k + 1 < n_items:
+                sort(k + 1)
+            run(AFTER_QUANTISE.get(back, ""))
+            if k >= 1:
+                multiply(k - 1)
+            run(AFTER_MULTIPLY.get(back, ""))

@@ -38,7 +38,7 @@ SCALAR_COLS = 32
 FLOPS = 2 * BATCH * IMAGE * K * CHANNELS
 
 TILE_END_CHUNKS = 0
-TILE_MAJOR = (0,)
+TILE_MAJOR = (0, 14, 15)
 SPLITS = {0: 4}
 W_PIECES = {}
 SCALES_FIRST = False
@@ -48,10 +48,11 @@ CONST_AFTER = 0
 H_BUFS = 10
 W_BUFS = 5
 SORT_BUFS = 2
-STORE_EVERY = 4
+STORE_EVERY = 1
 AFTER_TURN = {}
-AFTER_QUANTISE = {}
-AFTER_MULTIPLY = {0: "bias0 bias1 stats0 stats1 bias2 bias3 stats2 stats3 normv0 normv1 normv2 normv3 tout0 fin0 tout1 fin1 tout2 fin2 tout3 fin3"}
+AFTER_QUANTISE = {0: "biasS0 statsS0 biasS1 statsS1 gainS0 norms0 gainS1 norms1"}
+AFTER_MULTIPLY = {0: "biasS2 statsS2 toutI0 toutI1 bias3 stats3 gainS2 norms2 normv3 finI0 toutI2 toutI3 finI1"}
+SCALE_FORM = "chunk"
 
 
 def make_slabs():
@@ -97,6 +98,7 @@ def tile_transformerconvblock_pc_k_kernel(
         sort_pool = ctx.enter_context(tc.tile_pool(name="sort_pool", bufs=SORT_BUFS))
         work = ctx.enter_context(tc.tile_pool(name="work", bufs=2))
         tail = ctx.enter_context(tc.tile_pool(name="tail", bufs=TILES))
+        image_pool = ctx.enter_context(tc.tile_pool(name="image_pool", bufs=BATCH))
         acc_pool = ctx.enter_context(tc.psum_pool(name="acc_pool", bufs=1))
         turn_pool = ctx.enter_context(tc.psum_pool(name="turn_pool", bufs=4))
 
@@ -116,7 +118,7 @@ def tile_transformerconvblock_pc_k_kernel(
 
         w_planes = consts.tile([P, CHUNKS, CHANNELS], U8, align_bytes=64)
         nc.vector.memset(w_planes[:].bitcast(I32), 0)
-        x_rows = consts.tile([P, CHANNEL_TILES, BATCH, IMAGE], BF16)
+        x_rows = consts.tile([P, BATCH, CHANNEL_TILES, IMAGE], BF16)
 
         plan = []
         planned = set()
@@ -139,8 +141,8 @@ def tile_transformerconvblock_pc_k_kernel(
                             planned.add(("w", chunk, piece))
                             plan.append(("w", chunk, piece))
         if SCALES_FIRST:
-            where = [n for n, e in enumerate(plan) if e[0] == "w"][0]
-            plan[where:where] = [("s", chunk) for chunk in range(CHUNKS)]
+            where = [n for n, e in enumerate(plan) if e[0] == "w"][0] if SCALES_FIRST == "before W" else 0
+            plan[where:where] = [("s", -1)]
         for chunk, slab in MOVES:
             moved = [e for e in plan if e[0] in ("s", "w") and e[1] == chunk]
             plan = [e for e in plan if e not in moved]
@@ -183,6 +185,26 @@ def tile_transformerconvblock_pc_k_kernel(
                         out=by_tile[:, t0:t1, k0:k1],
                         in_=h_view[:, tiles[0] + t0 : tiles[0] + t1, first * K_PASS + k0 : first * K_PASS + k1],
                     )
+            elif kind == "s" and entry[1] < 0 and SCALE_FORM == "member":
+                for member in range(CHUNK_GROUPS):
+                    for quadrant in range(QUADRANTS):
+                        first = 32 * quadrant + QUADRANT_SCALES * member
+                        rows = slice(quadrant * QUADRANT_SCALES, (quadrant + 1) * QUADRANT_SCALES)
+                        nc.sync.dma_start(
+                            out=w_planes[first : first + QUADRANT_SCALES, :, :].bitcast(I32),
+                            in_=ffn2_w_scales[member::CHUNK_GROUPS, rows, :].rearrange("a r n -> r a n").bitcast(I32),
+                        )
+            elif kind == "s" and entry[1] < 0 and SCALE_FORM == "quadrant":
+                for quadrant in range(QUADRANTS):
+                    first = 32 * quadrant
+                    rows = slice(quadrant * QUADRANT_SCALES, (quadrant + 1) * QUADRANT_SCALES)
+                    nc.sync.dma_start(
+                        out=w_planes[first : first + CHUNK_GROUPS * QUADRANT_SCALES, :, :].bitcast(I32),
+                        in_=ffn2_w_scales[:, rows, :].rearrange("(a m) r n -> m r a n", m=CHUNK_GROUPS).bitcast(I32),
+                    )
+            elif kind == "s" and entry[1] < 0:
+                for chunk in range(CHUNKS):
+                    issue(("s", chunk))
             elif kind == "s":
                 chunk = entry[1]
                 groups = slice(chunk * CHUNK_GROUPS, (chunk + 1) * CHUNK_GROUPS)
@@ -207,7 +229,7 @@ def tile_transformerconvblock_pc_k_kernel(
                 )
             else:
                 b = entry[1]
-                nc.sync.dma_start(out=x_rows[:, :, b, :], in_=x[b].rearrange("(j c) i w -> c j (i w)", c=P))
+                nc.sync.dma_start(out=x_rows[:, b, :, :], in_=x[b].rearrange("(j c) i w -> c j (i w)", c=P))
 
         def pump():
             while state["next"] < len(plan):
@@ -229,6 +251,8 @@ def tile_transformerconvblock_pc_k_kernel(
         nc.vector.memset(ones[:], 1.0)
         one_col = consts.tile([P, 1], F32)
         nc.vector.memset(one_col[:], 1.0)
+        eps_col = consts.tile([P, 1], F32)
+        nc.scalar.activation(out=eps_col[:], in_=one_col[:], func=ACT.Copy, scale=EPS)
         sqrt_warm = consts.tile([P, 1], F32)
         nc.scalar.activation(out=sqrt_warm[:], in_=one_col[:], func=ACT.Sqrt)
 
@@ -238,6 +262,7 @@ def tile_transformerconvblock_pc_k_kernel(
         norm_scale = scalars[:, NORM_SCALE_COL : NORM_SCALE_COL + 1]
         ffn_scale_sq = consts.tile([P, 1], F32)
         ln_cols = consts.tile([P, 2 * CHANNEL_TILES], F32)
+        var_scale = consts.tile([P, 1], F32)
 
         def make_constants():
             bias_bank = turn_pool.tile([P, CHANNELS], F32, tag="turn")
@@ -249,6 +274,7 @@ def tile_transformerconvblock_pc_k_kernel(
             )
             nc.scalar.copy(out=scalars[:], in_=scalar_bank[:])
             nc.scalar.activation(out=ffn_scale_sq[:], in_=ffn_scale, func=ACT.Copy, scale=ffn_scale)
+            nc.scalar.activation(out=var_scale[:], in_=ffn_scale_sq[:], func=ACT.Copy, scale=1.0 / CHANNELS)
             ln_bank = turn_pool.tile([P, P], BF16, tag="turn")
             nc.tensor.transpose(ln_bank[:], ln_rows[:], ident_bf16[:])
             nc.scalar.activation(out=ln_cols[:], in_=ln_bank[:, 0 : 2 * CHANNEL_TILES], func=ACT.Copy, scale=norm_scale)
@@ -408,7 +434,7 @@ def tile_transformerconvblock_pc_k_kernel(
                     out=summed[:, j, :],
                     in0=turned_out[t][:, j, :],
                     scalar=ln_cols[:, j : j + 1],
-                    in1=x_rows[:, j, b, pixels],
+                    in1=x_rows[:, b, j, pixels],
                     op0=ALU.mult,
                     op1=ALU.add,
                 )
@@ -422,7 +448,70 @@ def tile_transformerconvblock_pc_k_kernel(
                     js = slice(j + 1 - STORE_EVERY, j + 1)
                     nc.sync.dma_start(out=out_view[:, js, pixels], in_=result[:, js, :])
 
-        stages = {"bias": bias, "stats": stats, "normv": normv, "gain": gain, "norms": norms, "tout": tout, "fin": fin}
+        sum_tiles = {}
+
+        def biasS(t):
+            biased = tail.tile([P, CHANNELS], F32, tag="biased")
+            sums = tail.tile([P, 4], F32, tag="sums")
+            nc.vector.scalar_tensor_tensor(
+                out=biased[:], in0=acc[t][:], scalar=1.0, in1=bias_all[:], op0=ALU.mult, op1=ALU.add, accum_out=sums[:, 0:1]
+            )
+            biased_tiles[t] = biased
+            sum_tiles[t] = sums
+
+        def statsS(t):
+            sums = sum_tiles[t]
+            nc.scalar.activation(out=sums[:, 1:2], in_=sums[:, 0:1], func=ACT.Copy, scale=-1.0 / CHANNELS)
+            squares = tail.tile([P, CHANNELS], F32, tag="unit")
+            nc.scalar.activation(
+                out=squares[:], in_=biased_tiles[t][:], func=ACT.Square, bias=sums[:, 1:2], accum_out=sums[:, 2:3]
+            )
+            nc.scalar.activation(out=sums[:, 3:4], in_=sums[:, 2:3], func=ACT.Sqrt, scale=var_scale[:], bias=eps_col[:])
+
+        def gainS(t):
+            sums = sum_tiles[t]
+            pair = tail.tile([P, 2], F32, tag="pair")
+            nc.vector.reciprocal(out=pair[:, 0:1], in_=sums[:, 3:4])
+            nc.vector.tensor_tensor(out=pair[:, 1:2], in0=sums[:, 1:2], in1=pair[:, 0:1], op=ALU.mult)
+            gain_tiles[t] = pair
+
+        image_banks = {}
+
+        def toutI(t):
+            b, half = divmod(t, IMAGE_TILES)
+            if b not in image_banks:
+                bank_a = acc_pool.tile([P, 2, IMAGE], F32, name="acc%d" % (IMAGE_TILES * b))
+                bank_b = acc_pool.tile([P, 2, IMAGE], F32, name="acc%d" % (IMAGE_TILES * b + 1))
+                image_banks[b] = (bank_a, bank_b)
+            for j in range(CHANNEL_TILES):
+                nc.tensor.transpose(
+                    image_banks[b][j // 2][:, j % 2, half * P : (half + 1) * P], unit_tiles[t][:, j * P : (j + 1) * P], ident_f32[:]
+                )
+
+        def finI(b):
+            out_view = out[b].rearrange("(j c) i w -> c j (i w)", c=P)
+            summed = image_pool.tile([P, CHANNEL_TILES, IMAGE], F32, tag="summedI")
+            result = image_pool.tile([P, CHANNEL_TILES, IMAGE], F32, tag="resultI")
+            for j in range(CHANNEL_TILES):
+                nc.vector.scalar_tensor_tensor(
+                    out=summed[:, j, :],
+                    in0=image_banks[b][j // 2][:, j % 2, :],
+                    scalar=ln_cols[:, j : j + 1],
+                    in1=x_rows[:, b, j, :],
+                    op0=ALU.mult,
+                    op1=ALU.add,
+                )
+                nc.scalar.activation(
+                    out=result[:, j, :],
+                    in_=summed[:, j, :],
+                    func=ACT.Relu,
+                    bias=ln_cols[:, CHANNEL_TILES + j : CHANNEL_TILES + j + 1],
+                )
+                if j % STORE_EVERY == STORE_EVERY - 1:
+                    js = slice(j + 1 - STORE_EVERY, j + 1)
+                    nc.sync.dma_start(out=out_view[:, js, :], in_=result[:, js, :])
+
+        stages = {"biasS": biasS, "statsS": statsS, "gainS": gainS, "toutI": toutI, "finI": finI, "bias": bias, "stats": stats, "normv": normv, "gain": gain, "norms": norms, "tout": tout, "fin": fin}
 
         def run(names):
             for name in names.split():

@@ -44,7 +44,7 @@ W_PIECES = {}
 SCALES_FIRST = False
 MOVES = []
 X_BEFORE = (0, 0)
-CONST_AFTER = 0
+CONST_AFTER = 1
 H_BUFS = 10
 W_BUFS = 5
 SORT_BUFS = 2
@@ -53,6 +53,16 @@ AFTER_TURN = {}
 AFTER_QUANTISE = {0: "biasS0 statsS0 biasS1 statsS1 gainS0 norms0 gainS1 norms1"}
 AFTER_MULTIPLY = {0: "biasS2 statsS2 toutI0 toutI1 bias3 stats3 gainS2 norms2 normv3 finI0 toutI2 toutI3 finI1"}
 SCALE_FORM = "chunk"
+SORT_SPLIT = 1
+PROBE_LOADS_BEFORE = ()
+FINAL_BY_GROUP = False
+H_ON_SCALAR = ()
+MX_ALIGN = 64
+N_WARM = 0
+SMALL_LOADS_BEFORE = 2
+W_BEFORE_SCALES = True
+CONST_BANKS = "turn"
+RSQRT = False
 
 
 def make_slabs():
@@ -108,15 +118,20 @@ def tile_transformerconvblock_pc_k_kernel(
         nc.vector.memset(ln_rows[:], 0.0)
         ffn_col = CHANNELS + FFN_SCALE_COL
         norm_col = CHANNELS + NORM_SCALE_COL
-        nc.scalar.dma_start(out=one_row[0:1, 0:CHANNELS], in_=ffn2_b.unsqueeze(0))
-        nc.scalar.dma_start(out=one_row[0:1, ffn_col : ffn_col + 1], in_=scale_ffn.unsqueeze(0))
-        nc.scalar.dma_start(out=one_row[0:1, norm_col : norm_col + 1], in_=scale_norm2.unsqueeze(0))
-        nc.scalar.dma_start(out=ln_rows[0:CHANNEL_TILES, :], in_=ln2_w.rearrange("(j c) -> j c", c=P))
-        nc.scalar.dma_start(
-            out=ln_rows[CHANNEL_TILES : 2 * CHANNEL_TILES, :], in_=ln2_b.rearrange("(j c) -> j c", c=P)
-        )
 
-        w_planes = consts.tile([P, CHUNKS, CHANNELS], U8, align_bytes=64)
+        def small_loads(queue):
+            queue.dma_start(out=one_row[0:1, 0:CHANNELS], in_=ffn2_b.unsqueeze(0))
+            queue.dma_start(out=one_row[0:1, ffn_col : ffn_col + 1], in_=scale_ffn.unsqueeze(0))
+            queue.dma_start(out=one_row[0:1, norm_col : norm_col + 1], in_=scale_norm2.unsqueeze(0))
+            queue.dma_start(out=ln_rows[0:CHANNEL_TILES, :], in_=ln2_w.rearrange("(j c) -> j c", c=P))
+            queue.dma_start(
+                out=ln_rows[CHANNEL_TILES : 2 * CHANNEL_TILES, :], in_=ln2_b.rearrange("(j c) -> j c", c=P)
+            )
+
+        if SMALL_LOADS_BEFORE is None:
+            small_loads(nc.scalar)
+
+        w_planes = consts.tile([P, CHUNKS, CHANNELS], U8, align_bytes=MX_ALIGN)
         nc.vector.memset(w_planes[:].bitcast(I32), 0)
         x_rows = consts.tile([P, BATCH, CHANNEL_TILES, IMAGE], BF16)
 
@@ -134,12 +149,15 @@ def tile_transformerconvblock_pc_k_kernel(
                         last_use[chunk] = k - 1
                         pieces = W_PIECES.get(chunk, 1)
                         piece = (g % CHUNK_GROUPS) * pieces // CHUNK_GROUPS
-                        if ("s", chunk) not in planned and not SCALES_FIRST:
+                        if ("s", chunk) not in planned and not SCALES_FIRST and not W_BEFORE_SCALES:
                             planned.add(("s", chunk))
                             plan.append(("s", chunk))
                         if ("w", chunk, piece) not in planned:
                             planned.add(("w", chunk, piece))
                             plan.append(("w", chunk, piece))
+                        if ("s", chunk) not in planned and not SCALES_FIRST:
+                            planned.add(("s", chunk))
+                            plan.append(("s", chunk))
         if SCALES_FIRST:
             where = [n for n, e in enumerate(plan) if e[0] == "w"][0] if SCALES_FIRST == "before W" else 0
             plan[where:where] = [("s", -1)]
@@ -156,6 +174,11 @@ def tile_transformerconvblock_pc_k_kernel(
             else:
                 plan.append(("x", b))
 
+        for n, slab in enumerate(PROBE_LOADS_BEFORE):
+            where = [m for m, e in enumerate(plan) if e[0] == "h" and e[1] == slab][0]
+            plan[where:where] = [("d", n)]
+        if SMALL_LOADS_BEFORE is not None:
+            plan[SMALL_LOADS_BEFORE:SMALL_LOADS_BEFORE] = [("c",)]
         h_tiles = {}
         w_tiles = {}
         state = {"next": 0, "sorted": 0, "chunks": 0}
@@ -180,11 +203,19 @@ def tile_transformerconvblock_pc_k_kernel(
                     per_bank = width // per_tile
                     assert j0 // per_tile == (j1 - 1) // per_tile
                     spans = [(j0 // per_tile, j0 // per_tile + 1, (j0 % per_tile) * per_bank, (j0 % per_tile + j1 - j0) * per_bank)]
+                queue = nc.scalar if i in H_ON_SCALAR else nc.sync
                 for t0, t1, k0, k1 in spans:
-                    nc.sync.dma_start(
+                    queue.dma_start(
                         out=by_tile[:, t0:t1, k0:k1],
                         in_=h_view[:, tiles[0] + t0 : tiles[0] + t1, first * K_PASS + k0 : first * K_PASS + k1],
                     )
+            elif kind == "c":
+                small_loads(nc.sync)
+            elif kind == "d":
+                probe = consts.tile([P, SLAB_K], BF16, name="probe%d" % entry[1])
+                nc.sync.dma_start(
+                    out=probe[:].rearrange("p (t k) -> p t k", t=SLOTS), in_=h_view[:, 0:SLOTS, 0 : SLAB_K // SLOTS]
+                )
             elif kind == "s" and entry[1] < 0 and SCALE_FORM == "member":
                 for member in range(CHUNK_GROUPS):
                     for quadrant in range(QUADRANTS):
@@ -218,7 +249,7 @@ def tile_transformerconvblock_pc_k_kernel(
             elif kind == "w":
                 chunk, piece = entry[1:]
                 if chunk not in w_tiles:
-                    w_words = w_pool.tile([P, CHUNK_GROUPS, PACK * CHANNELS], U8, tag="w_words", align_bytes=64)
+                    w_words = w_pool.tile([P, CHUNK_GROUPS, PACK * CHANNELS], U8, tag="w_words", align_bytes=MX_ALIGN)
                     w_tiles[chunk] = w_words
                 per = CHUNK_GROUPS // W_PIECES.get(chunk, 1)
                 nc.sync.dma_start(
@@ -254,7 +285,14 @@ def tile_transformerconvblock_pc_k_kernel(
         eps_col = consts.tile([P, 1], F32)
         nc.scalar.activation(out=eps_col[:], in_=one_col[:], func=ACT.Copy, scale=EPS)
         sqrt_warm = consts.tile([P, 1], F32)
-        nc.scalar.activation(out=sqrt_warm[:], in_=one_col[:], func=ACT.Sqrt)
+        nc.scalar.activation(out=sqrt_warm[:], in_=one_col[:], func=ACT.Abs_reciprocal_sqrt if RSQRT else ACT.Sqrt)
+
+        if N_WARM:
+            warm_in = consts.tile([P, CHANNELS], BF16)
+            nc.vector.memset(warm_in[:], 0.0)
+            for n in range(N_WARM):
+                warm_bank = turn_pool.tile([P, CHANNELS], F32, tag="turn")
+                nc.tensor.matmul(out=warm_bank[:], lhsT=ones[:], rhs=warm_in[:], start=True, stop=True)
 
         bias_all = consts.tile([P, CHANNELS], F32)
         scalars = consts.tile([P, SCALAR_COLS], F32)
@@ -265,24 +303,34 @@ def tile_transformerconvblock_pc_k_kernel(
         var_scale = consts.tile([P, 1], F32)
 
         def make_constants():
-            bias_bank = turn_pool.tile([P, CHANNELS], F32, tag="turn")
-            nc.tensor.matmul(out=bias_bank[:], lhsT=ones[:], rhs=one_row[:, 0:CHANNELS], start=True, stop=True)
-            nc.scalar.copy(out=bias_all[:], in_=bias_bank[:])
-            scalar_bank = turn_pool.tile([P, SCALAR_COLS], F32, tag="turn")
+            if CONST_BANKS == "acc":
+                assert 2 not in acc and 3 not in acc
+                scalar_bank = acc_pool.tile([P, SCALAR_COLS], F32, name="acc2")
+            else:
+                scalar_bank = turn_pool.tile([P, SCALAR_COLS], F32, tag="turn")
             nc.tensor.matmul(
                 out=scalar_bank[:], lhsT=ones[:], rhs=one_row[:, CHANNELS : CHANNELS + SCALAR_COLS], start=True, stop=True
             )
             nc.scalar.copy(out=scalars[:], in_=scalar_bank[:])
+            if CONST_BANKS == "acc":
+                bias_bank = acc_pool.tile([P, CHANNELS], F32, name="acc3")
+            else:
+                bias_bank = turn_pool.tile([P, CHANNELS], F32, tag="turn")
+            nc.tensor.matmul(out=bias_bank[:], lhsT=ones[:], rhs=one_row[:, 0:CHANNELS], start=True, stop=True)
+            nc.scalar.copy(out=bias_all[:], in_=bias_bank[:])
             nc.scalar.activation(out=ffn_scale_sq[:], in_=ffn_scale, func=ACT.Copy, scale=ffn_scale)
             nc.scalar.activation(out=var_scale[:], in_=ffn_scale_sq[:], func=ACT.Copy, scale=1.0 / CHANNELS)
-            ln_bank = turn_pool.tile([P, P], BF16, tag="turn")
+            if CONST_BANKS == "acc":
+                ln_bank = acc_pool.tile([P, P], BF16, name="acc2")
+            else:
+                ln_bank = turn_pool.tile([P, P], BF16, tag="turn")
             nc.tensor.transpose(ln_bank[:], ln_rows[:], ident_bf16[:])
             nc.scalar.activation(out=ln_cols[:], in_=ln_bank[:, 0 : 2 * CHANNEL_TILES], func=ACT.Copy, scale=norm_scale)
             nc.scalar.activation(
                 out=ln_cols[:, 0:CHANNEL_TILES], in_=ln_cols[:, 0:CHANNEL_TILES], func=ACT.Copy, scale=ffn_scale
             )
 
-        acc = [acc_pool.tile([P, CHANNELS], F32, name="acc%d" % t) for t in range(TILES)]
+        acc = {}
 
         sorted_tiles = {}
         grouped_tiles = {}
@@ -305,7 +353,9 @@ def tile_transformerconvblock_pc_k_kernel(
                 source = h_words[:, j0 * per_bank : j1 * per_bank].rearrange(
                     "p (j s q u) -> p j s u q", j=j1 - j0, s=SLOTS, u=HALVES
                 )
-            nc.vector.tensor_copy(out=sorted_tiles[i][:, j0:j1, :, :, :], in_=source)
+            step = max(1, (j1 - j0) // SORT_SPLIT)
+            for a in range(0, j1 - j0, step):
+                nc.vector.tensor_copy(out=sorted_tiles[i][:, j0 + a : j0 + a + step, :, :, :], in_=source[:, a : a + step, :, :, :])
             if j1 == BANKS:
                 h_tiles.pop(i)
                 state["sorted"] += 1
@@ -314,7 +364,7 @@ def tile_transformerconvblock_pc_k_kernel(
         def turn(k):
             i, j0, j1 = items[k]
             if i not in grouped_tiles:
-                grouped = work.tile([P, BANKS, IMAGE * PACK], BF16, tag="grouped", align_bytes=64)
+                grouped = work.tile([P, BANKS, IMAGE * PACK], BF16, tag="grouped", align_bytes=MX_ALIGN)
                 grouped_tiles[i] = grouped
             grouped_words = grouped_tiles[i][:].bitcast(F32).rearrange("p j (x u) -> p j x u", u=HALVES)
             for j in range(j0, j1):
@@ -329,8 +379,8 @@ def tile_transformerconvblock_pc_k_kernel(
         def quantise(k):
             i, j0, j1 = items[k]
             if i not in code_tiles:
-                h_codes = work.tile([P, BANKS, IMAGE], U32, tag="h_codes", align_bytes=64)
-                h_planes = work.tile([P, BANKS, IMAGE], U8, tag="h_planes", align_bytes=64)
+                h_codes = work.tile([P, BANKS, IMAGE], U32, tag="h_codes", align_bytes=MX_ALIGN)
+                h_planes = work.tile([P, BANKS, IMAGE], U8, tag="h_planes", align_bytes=MX_ALIGN)
                 code_tiles[i] = (h_codes, h_planes)
             h_codes, h_planes = code_tiles[i]
             for j in range(j0, j1):
@@ -340,13 +390,16 @@ def tile_transformerconvblock_pc_k_kernel(
             if j1 == BANKS:
                 grouped_tiles.pop(i)
 
-        def multiply(k):
+        def multiply(k, banks=None):
             i, j0, j1 = items[k]
             h_codes, h_planes = code_tiles[i]
-            for j in range(j0, j1):
+            for j in range(j0, j1) if banks is None else banks:
                 for s, (t, g) in enumerate(units_of_bank(i, slabs[i], j)):
                     chunk, member = divmod(g, CHUNK_GROUPS)
                     pixels = slice(s * P, (s + 1) * P)
+                    if t not in acc:
+                        bank = acc_pool.tile([P, CHANNELS], F32, name="acc%d" % t)
+                        acc[t] = bank
                     nc.tensor.matmul_mx(
                         out=acc[t][:],
                         lhsT=h_codes[:, j, pixels].bitcast(FP8X4),
@@ -356,6 +409,8 @@ def tile_transformerconvblock_pc_k_kernel(
                         start=(g == 0),
                         stop=(g == GROUPS - 1),
                     )
+            if banks is not None:
+                return
             if j1 == BANKS:
                 code_tiles.pop(i)
             freed = [chunk for chunk in last_use if last_use[chunk] == k]
@@ -381,16 +436,24 @@ def tile_transformerconvblock_pc_k_kernel(
             mean_var = tail.tile([P, 2], F32, tag="mean_var")
             nc.vector.bn_aggr(out=mean_var[:], in_=stat[:])
             spread = tail.tile([P, 1], F32, tag="spread")
-            nc.vector.tensor_scalar(
-                out=spread[:], in0=mean_var[:, 1:2], scalar1=ffn_scale_sq[:], scalar2=EPS, op0=ALU.mult, op1=ALU.add
-            )
-            nc.scalar.activation(out=spread[:], in_=spread[:], func=ACT.Sqrt)
+            if RSQRT:
+                nc.scalar.activation(
+                    out=spread[:], in_=mean_var[:, 1:2], func=ACT.Abs_reciprocal_sqrt, scale=ffn_scale_sq[:], bias=eps_col[:]
+                )
+            else:
+                nc.vector.tensor_scalar(
+                    out=spread[:], in0=mean_var[:, 1:2], scalar1=ffn_scale_sq[:], scalar2=EPS, op0=ALU.mult, op1=ALU.add
+                )
+                nc.scalar.activation(out=spread[:], in_=spread[:], func=ACT.Sqrt)
             mean_var_tiles[t] = mean_var
             spread_tiles[t] = spread
 
         def normv(t):
-            gain = tail.tile([P, 1], F32, tag="gain")
-            nc.vector.reciprocal(out=gain[:], in_=spread_tiles[t][:])
+            if RSQRT:
+                gain = spread_tiles[t]
+            else:
+                gain = tail.tile([P, 1], F32, tag="gain")
+                nc.vector.reciprocal(out=gain[:], in_=spread_tiles[t][:])
             unit = tail.tile([P, CHANNELS], F32, tag="unit")
             nc.vector.tensor_scalar(
                 out=unit[:],
@@ -466,9 +529,19 @@ def tile_transformerconvblock_pc_k_kernel(
             nc.scalar.activation(
                 out=squares[:], in_=biased_tiles[t][:], func=ACT.Square, bias=sums[:, 1:2], accum_out=sums[:, 2:3]
             )
-            nc.scalar.activation(out=sums[:, 3:4], in_=sums[:, 2:3], func=ACT.Sqrt, scale=var_scale[:], bias=eps_col[:])
+            if RSQRT:
+                pair = tail.tile([P, 2], F32, tag="pair")
+                nc.scalar.activation(
+                    out=pair[:, 0:1], in_=sums[:, 2:3], func=ACT.Abs_reciprocal_sqrt, scale=var_scale[:], bias=eps_col[:]
+                )
+                nc.scalar.activation(out=pair[:, 1:2], in_=sums[:, 1:2], func=ACT.Copy, scale=pair[:, 0:1])
+                gain_tiles[t] = pair
+            else:
+                nc.scalar.activation(out=sums[:, 3:4], in_=sums[:, 2:3], func=ACT.Sqrt, scale=var_scale[:], bias=eps_col[:])
 
         def gainS(t):
+            if RSQRT:
+                return
             sums = sum_tiles[t]
             pair = tail.tile([P, 2], F32, tag="pair")
             nc.vector.reciprocal(out=pair[:, 0:1], in_=sums[:, 3:4])
@@ -518,6 +591,8 @@ def tile_transformerconvblock_pc_k_kernel(
                 stages[name[:-1]](int(name[-1]))
 
         sort(0)
+        if CONST_AFTER < 0:
+            make_constants()
         for k in range(n_items + 1):
             back = k - n_items
             if k < n_items:
@@ -530,6 +605,10 @@ def tile_transformerconvblock_pc_k_kernel(
             if k + 1 < n_items:
                 sort(k + 1)
             run(AFTER_QUANTISE.get(back, ""))
-            if k >= 1:
+            if k >= 1 and FINAL_BY_GROUP and back == 0:
+                for j in range(BANKS):
+                    multiply(k - 2, [j])
+                    multiply(k - 1, [j])
+            elif k >= 1 and not (FINAL_BY_GROUP and back == -1):
                 multiply(k - 1)
             run(AFTER_MULTIPLY.get(back, ""))

@@ -50,8 +50,8 @@ W_BUFS = 5
 SORT_BUFS = 2
 STORE_EVERY = 1
 AFTER_TURN = {}
-AFTER_QUANTISE = {0: "biasS0 statsS0 biasS1 statsS1 gainS0 norms0 gainS1 norms1"}
-AFTER_MULTIPLY = {0: "biasS2 statsS2 toutI0 toutI1 bias3 stats3 gainS2 norms2 normv3 finI0 toutI2 toutI3 finI1"}
+AFTER_QUANTISE = {0: "biasS0 statsS0 biasS1 statsS1 norms0 norms1"}
+AFTER_MULTIPLY = {0: "biasS2 statsS2 toutI0 toutI1 bias3 stats3 norms2 normv3 finI0 toutI2 toutI3 finI1"}
 SCALE_FORM = "chunk"
 SORT_SPLIT = 1
 PROBE_LOADS_BEFORE = ()
@@ -62,7 +62,7 @@ N_WARM = 0
 SMALL_LOADS_BEFORE = 2
 W_BEFORE_SCALES = True
 CONST_BANKS = "turn"
-RSQRT = False
+RSQRT = True
 
 
 def make_slabs():

@@ -50,10 +50,10 @@ W_BUFS = 5
 SORT_BUFS = 2
 STORE_EVERY = 1
 AFTER_TURN = {}
-AFTER_QUANTISE = {0: "biasS0 statsS0 biasS1 statsS1 norms0 norms1"}
-AFTER_MULTIPLY = {0: "biasS2 statsS2 toutI0 toutI1 bias3 stats3 norms2 normv3 finI0 toutI2 toutI3 finI1"}
+AFTER_QUANTISE = {0: "biasS0 statsS0 biasS1 statsS1"}
+AFTER_MULTIPLY = {0: "biasS2 normV0 normV1 statsS2 norms2 toutI0 toutI1 bias3 stats3 toutI2 finA0 normv3 finB0 toutI3 finA1 finB1"}
 SCALE_FORM = "chunk"
-SORT_SPLIT = 1
+SORT_SPLIT = 2
 PROBE_LOADS_BEFORE = ()
 FINAL_BY_GROUP = False
 H_ON_SCALAR = ()
@@ -63,10 +63,34 @@ SMALL_LOADS_BEFORE = 2
 W_BEFORE_SCALES = True
 CONST_BANKS = "turn"
 RSQRT = True
+PAIR_FROM = None
+PAIR_TO = None
+POOL_SCALES_FROM = None
+PAIR_STARTS = ()
+VECTOR_BANKS = ()
+CODE_BUFS = 2
+SORT_SPLITS = {}
+WARM_BEFORE_TURN = {}
+WARM_BEFORE_MULTIPLY = {}
+FINAL_BY_HALF = False
+SCALES_AHEAD = False
+RELU_ON_VECTOR = ()
+QUANT_BANKS = {1: 2, 2: 2, 3: 2, 4: 2, 5: 2, 6: 2, 7: 2, 8: 2, 9: 2, 10: 2, 11: 2, 12: 2, 13: 2, 14: 2}
 
 
 def make_slabs():
     slabs = []
+    if PAIR_FROM is not None:
+        for chunk in range(PAIR_FROM):
+            for b in range(BATCH):
+                slabs.append(((IMAGE_TILES * b, IMAGE_TILES * b + 1), chunk * CHUNK_GROUPS, CHUNK_GROUPS))
+        for chunk in range(PAIR_FROM, PAIR_TO, 2):
+            for t in range(TILES):
+                slabs.append(((t,), chunk * CHUNK_GROUPS, 2 * CHUNK_GROUPS))
+        for chunk in range(PAIR_TO, CHUNKS):
+            for b in range(BATCH):
+                slabs.append(((IMAGE_TILES * b, IMAGE_TILES * b + 1), chunk * CHUNK_GROUPS, CHUNK_GROUPS))
+        return slabs
     image_chunks = CHUNKS - TILE_END_CHUNKS
     for chunk in range(image_chunks):
         for b in range(BATCH):
@@ -107,6 +131,7 @@ def tile_transformerconvblock_pc_k_kernel(
         w_pool = ctx.enter_context(tc.tile_pool(name="w_pool", bufs=W_BUFS))
         sort_pool = ctx.enter_context(tc.tile_pool(name="sort_pool", bufs=SORT_BUFS))
         work = ctx.enter_context(tc.tile_pool(name="work", bufs=2))
+        code_pool = ctx.enter_context(tc.tile_pool(name="code_pool", bufs=CODE_BUFS))
         tail = ctx.enter_context(tc.tile_pool(name="tail", bufs=TILES))
         image_pool = ctx.enter_context(tc.tile_pool(name="image_pool", bufs=BATCH))
         acc_pool = ctx.enter_context(tc.psum_pool(name="acc_pool", bufs=1))
@@ -179,6 +204,13 @@ def tile_transformerconvblock_pc_k_kernel(
             plan[where:where] = [("d", n)]
         if SMALL_LOADS_BEFORE is not None:
             plan[SMALL_LOADS_BEFORE:SMALL_LOADS_BEFORE] = [("c",)]
+        if SCALES_AHEAD:
+            for chunk in range(1, CHUNKS):
+                plan.remove(("s", chunk))
+                where = max(n for n, e in enumerate(plan) if e[0] == "h" and e[1] == 2 * chunk - 1)
+                plan[where + 1 : where + 1] = [("s", chunk)]
+        pool_scales = [e for e in plan if e[0] == "s" and POOL_SCALES_FROM is not None and e[1] >= POOL_SCALES_FROM]
+        plan = [e for e in plan if e not in pool_scales]
         h_tiles = {}
         w_tiles = {}
         state = {"next": 0, "sorted": 0, "chunks": 0}
@@ -239,12 +271,13 @@ def tile_transformerconvblock_pc_k_kernel(
             elif kind == "s":
                 chunk = entry[1]
                 groups = slice(chunk * CHUNK_GROUPS, (chunk + 1) * CHUNK_GROUPS)
+                on_pool = POOL_SCALES_FROM is not None and chunk >= POOL_SCALES_FROM
                 for quadrant in range(QUADRANTS):
                     first = 32 * quadrant
                     rows = slice(quadrant * QUADRANT_SCALES, (quadrant + 1) * QUADRANT_SCALES)
-                    nc.sync.dma_start(
-                        out=w_planes[first : first + CHUNK_GROUPS * QUADRANT_SCALES, chunk, :].bitcast(I32),
-                        in_=ffn2_w_scales[groups, rows, :].bitcast(I32),
+                    (nc.gpsimd if on_pool else nc.sync).dma_start(
+                        out=w_planes[first : first + CHUNK_GROUPS * QUADRANT_SCALES, chunk, :].bitcast(F32 if on_pool else I32),
+                        in_=ffn2_w_scales[groups, rows, :].bitcast(F32 if on_pool else I32),
                     )
             elif kind == "w":
                 chunk, piece = entry[1:]
@@ -278,6 +311,8 @@ def tile_transformerconvblock_pc_k_kernel(
         make_identity(nc, ident_f32[:])
         ident_bf16 = consts.tile([P, P], BF16)
         make_identity(nc, ident_bf16[:])
+        for entry in pool_scales:
+            issue(entry)
         ones = consts.tile([P, P], BF16)
         nc.vector.memset(ones[:], 1.0)
         one_col = consts.tile([P, 1], F32)
@@ -287,12 +322,22 @@ def tile_transformerconvblock_pc_k_kernel(
         sqrt_warm = consts.tile([P, 1], F32)
         nc.scalar.activation(out=sqrt_warm[:], in_=one_col[:], func=ACT.Abs_reciprocal_sqrt if RSQRT else ACT.Sqrt)
 
-        if N_WARM:
-            warm_in = consts.tile([P, CHANNELS], BF16)
-            nc.vector.memset(warm_in[:], 0.0)
-            for n in range(N_WARM):
-                warm_bank = turn_pool.tile([P, CHANNELS], F32, tag="turn")
-                nc.tensor.matmul(out=warm_bank[:], lhsT=ones[:], rhs=warm_in[:], start=True, stop=True)
+        acc = {}
+        warm_tiles = {}
+
+        def warm(n):
+            if not n:
+                return
+            if not warm_tiles:
+                warm_in = consts.tile([P, CHANNELS], BF16)
+                nc.vector.memset(warm_in[:], 0.0)
+                warm_bank = acc_pool.tile([P, CHANNELS], F32, name="acc3")
+                warm_tiles[0] = (warm_in, warm_bank)
+            assert 3 not in acc
+            for m in range(n):
+                nc.tensor.matmul(out=warm_tiles[0][1][:], lhsT=ones[:], rhs=warm_tiles[0][0][:], start=True, stop=True)
+
+        warm(N_WARM)
 
         bias_all = consts.tile([P, CHANNELS], F32)
         scalars = consts.tile([P, SCALAR_COLS], F32)
@@ -330,13 +375,17 @@ def tile_transformerconvblock_pc_k_kernel(
                 out=ln_cols[:, 0:CHANNEL_TILES], in_=ln_cols[:, 0:CHANNEL_TILES], func=ACT.Copy, scale=ffn_scale
             )
 
-        acc = {}
 
         sorted_tiles = {}
         grouped_tiles = {}
         code_tiles = {}
 
+        done = set()
+
         def sort(k):
+            if ("sort", k) in done:
+                return
+            done.add(("sort", k))
             i, j0, j1 = items[k]
             tiles = slabs[i][0]
             if i not in sorted_tiles:
@@ -353,7 +402,7 @@ def tile_transformerconvblock_pc_k_kernel(
                 source = h_words[:, j0 * per_bank : j1 * per_bank].rearrange(
                     "p (j s q u) -> p j s u q", j=j1 - j0, s=SLOTS, u=HALVES
                 )
-            step = max(1, (j1 - j0) // SORT_SPLIT)
+            step = max(1, (j1 - j0) // SORT_SPLITS.get(i, SORT_SPLIT))
             for a in range(0, j1 - j0, step):
                 nc.vector.tensor_copy(out=sorted_tiles[i][:, j0 + a : j0 + a + step, :, :, :], in_=source[:, a : a + step, :, :, :])
             if j1 == BANKS:
@@ -361,7 +410,7 @@ def tile_transformerconvblock_pc_k_kernel(
                 state["sorted"] += 1
                 pump()
 
-        def turn(k):
+        def turn(k, by_vector=()):
             i, j0, j1 = items[k]
             if i not in grouped_tiles:
                 grouped = work.tile([P, BANKS, IMAGE * PACK], BF16, tag="grouped", align_bytes=MX_ALIGN)
@@ -372,20 +421,29 @@ def tile_transformerconvblock_pc_k_kernel(
                 for s in range(SLOTS):
                     for u in range(HALVES):
                         nc.tensor.transpose(turned[:, u, s * P : (s + 1) * P], sorted_tiles[i][:, j, s, u, :], ident_f32[:])
-                nc.scalar.copy(out=grouped_words[:, j, :, :], in_=turned[:].rearrange("p u x -> p x u"))
+                if j in by_vector:
+                    nc.vector.tensor_copy(out=grouped_words[:, j, :, :], in_=turned[:].rearrange("p u x -> p x u"))
+                else:
+                    nc.scalar.copy(out=grouped_words[:, j, :, :], in_=turned[:].rearrange("p u x -> p x u"))
             if j1 == BANKS:
                 sorted_tiles.pop(i)
 
         def quantise(k):
+            if ("quantise", k) in done:
+                return
+            done.add(("quantise", k))
             i, j0, j1 = items[k]
             if i not in code_tiles:
-                h_codes = work.tile([P, BANKS, IMAGE], U32, tag="h_codes", align_bytes=MX_ALIGN)
-                h_planes = work.tile([P, BANKS, IMAGE], U8, tag="h_planes", align_bytes=MX_ALIGN)
+                h_codes = code_pool.tile([P, BANKS, IMAGE], U32, tag="h_codes", align_bytes=MX_ALIGN)
+                h_planes = code_pool.tile([P, BANKS, IMAGE], U8, tag="h_planes", align_bytes=MX_ALIGN)
                 code_tiles[i] = (h_codes, h_planes)
             h_codes, h_planes = code_tiles[i]
-            for j in range(j0, j1):
+            step = QUANT_BANKS.get(i, 1) if j1 - j0 == BANKS else 1
+            for j in range(j0, j1, step):
                 nc.vector.quantize_mx(
-                    out=h_codes[:, j, :].bitcast(FP8X4), scales=h_planes[:, j, :], in_=grouped_tiles[i][:, j, :]
+                    out=h_codes[:, j : j + step, :].rearrange("p j x -> p (j x)").bitcast(FP8X4),
+                    scales=h_planes[:, j : j + step, :].rearrange("p j x -> p (j x)"),
+                    in_=grouped_tiles[i][:, j : j + step, :].rearrange("p j x -> p (j x)"),
                 )
             if j1 == BANKS:
                 grouped_tiles.pop(i)
@@ -584,7 +642,66 @@ def tile_transformerconvblock_pc_k_kernel(
                     js = slice(j + 1 - STORE_EVERY, j + 1)
                     nc.sync.dma_start(out=out_view[:, js, :], in_=result[:, js, :])
 
-        stages = {"biasS": biasS, "statsS": statsS, "gainS": gainS, "toutI": toutI, "finI": finI, "bias": bias, "stats": stats, "normv": normv, "gain": gain, "norms": norms, "tout": tout, "fin": fin}
+        def normV(t):
+            unit = tail.tile([P, CHANNELS], F32, tag="unit")
+            nc.vector.tensor_scalar(
+                out=unit[:],
+                in0=biased_tiles[t][:],
+                scalar1=gain_tiles[t][:, 0:1],
+                scalar2=gain_tiles[t][:, 1:2],
+                op0=ALU.mult,
+                op1=ALU.add,
+            )
+            unit_tiles[t] = unit
+
+        last_tiles = {}
+
+        def last_stage(b, js, pixels, store):
+            if b not in last_tiles:
+                summed = image_pool.tile([P, CHANNEL_TILES, IMAGE], F32, tag="summedI")
+                result = image_pool.tile([P, CHANNEL_TILES, IMAGE], F32, tag="resultI")
+                last_tiles[b] = (summed, result)
+            summed, result = last_tiles[b]
+            out_view = out[b].rearrange("(j c) i w -> c j (i w)", c=P)
+            for j in js:
+                nc.vector.scalar_tensor_tensor(
+                    out=summed[:, j, pixels],
+                    in0=image_banks[b][j // 2][:, j % 2, pixels],
+                    scalar=ln_cols[:, j : j + 1],
+                    in1=x_rows[:, b, j, pixels],
+                    op0=ALU.mult,
+                    op1=ALU.add,
+                )
+                if store and j in RELU_ON_VECTOR:
+                    nc.vector.tensor_scalar(
+                        out=result[:, j, pixels],
+                        in0=summed[:, j, pixels],
+                        scalar1=ln_cols[:, CHANNEL_TILES + j : CHANNEL_TILES + j + 1],
+                        scalar2=0.0,
+                        op0=ALU.add,
+                        op1=ALU.max,
+                    )
+                else:
+                    nc.scalar.activation(
+                        out=result[:, j, pixels],
+                        in_=summed[:, j, pixels],
+                        func=ACT.Relu,
+                        bias=ln_cols[:, CHANNEL_TILES + j : CHANNEL_TILES + j + 1],
+                    )
+                if store:
+                    nc.sync.dma_start(out=out_view[:, j : j + 1, :], in_=result[:, j : j + 1, :])
+
+        def finA(b):
+            last_stage(b, (0, 1), slice(0, IMAGE), True)
+
+        def finB(b):
+            last_stage(b, (2, 3), slice(0, IMAGE), True)
+
+        def finT(t):
+            b, half = divmod(t, IMAGE_TILES)
+            last_stage(b, range(CHANNEL_TILES), slice(half * P, (half + 1) * P), half == IMAGE_TILES - 1)
+
+        stages = {"normV": normV, "finA": finA, "finB": finB, "finT": finT, "biasS": biasS, "statsS": statsS, "gainS": gainS, "toutI": toutI, "finI": finI, "bias": bias, "stats": stats, "normv": normv, "gain": gain, "norms": norms, "tout": tout, "fin": fin}
 
         def run(names):
             for name in names.split():
@@ -595,6 +712,22 @@ def tile_transformerconvblock_pc_k_kernel(
             make_constants()
         for k in range(n_items + 1):
             back = k - n_items
+            if k - 1 in PAIR_STARTS:
+                continue
+            if k in PAIR_STARTS:
+                turn(k, VECTOR_BANKS)
+                turn(k + 1)
+                quantise(k - 1)
+                quantise(k)
+                multiply(k - 1)
+                if k + 2 < n_items:
+                    sort(k + 2)
+                quantise(k + 1)
+                if k + 3 < n_items and k + 2 in PAIR_STARTS:
+                    sort(k + 3)
+                multiply(k)
+                continue
+            warm(WARM_BEFORE_TURN.get(k, 0))
             if k < n_items:
                 turn(k)
             if k == CONST_AFTER:
@@ -604,11 +737,20 @@ def tile_transformerconvblock_pc_k_kernel(
                 quantise(k - 1)
             if k + 1 < n_items:
                 sort(k + 1)
+            if k + 1 in PAIR_STARTS:
+                sort(k + 2)
             run(AFTER_QUANTISE.get(back, ""))
-            if k >= 1 and FINAL_BY_GROUP and back == 0:
+            if k >= 1 and FINAL_BY_HALF and back == 0:
+                for half in range(2):
+                    for item in (k - 2, k - 1):
+                        multiply(item, [half, 2 + half])
+            elif k >= 1 and FINAL_BY_HALF and back == -1:
+                pass
+            elif k >= 1 and FINAL_BY_GROUP and back == 0:
                 for j in range(BANKS):
                     multiply(k - 2, [j])
                     multiply(k - 1, [j])
             elif k >= 1 and not (FINAL_BY_GROUP and back == -1):
+                warm(WARM_BEFORE_MULTIPLY.get(k - 1, 0))
                 multiply(k - 1)
             run(AFTER_MULTIPLY.get(back, ""))

from contextlib import ExitStack

import concourse.mybir as mybir
from concourse.masks import make_identity

F32 = mybir.dt.float32
BF16 = mybir.dt.bfloat16
I32 = mybir.dt.int32
U32 = mybir.dt.uint32
U8 = mybir.dt.uint8
FP8X4 = mybir.dt.float8_e4m3fn_x4
ALU = mybir.AluOpType
ACT = mybir.ActivationFunctionType

P = 128
PACK = 4
K_PASS = P * PACK
HALVES = 2
BATCH = 2
IMAGE = 256
IMAGE_TILES = 2
TILES = 4
CHANNELS = 512
CHANNEL_TILES = 4
K = 16384
GROUPS = K // K_PASS
CHUNK_GROUPS = 4
CHUNKS = GROUPS // CHUNK_GROUPS
BANKS = 4
SLOTS = 2
SLAB_K = BANKS * SLOTS * K_PASS
QUADRANTS = 4
QUADRANT_SCALES = 4
EPS = 1e-5
FFN_SCALE_COL = 0
NORM_SCALE_COL = 16
SCALAR_COLS = 32
FLOPS = 2 * BATCH * IMAGE * K * CHANNELS

TILE_END_CHUNKS = 0
TILE_MAJOR = (0, 14, 15)
SPLITS = {0: 4}
W_PIECES = {}
SCALES_FIRST = False
MOVES = []
X_BEFORE = (0, 0)
CONST_AFTER = 1
H_BUFS = 10
W_BUFS = 5
SORT_BUFS = 2
STORE_EVERY = 1
AFTER_TURN = {}
AFTER_QUANTISE = {0: "biasS0 statsS0 biasS1 statsS1"}
AFTER_MULTIPLY = {0: "biasS2 normV0 normV1 statsS2 norms2 toutI0 toutI1 bias3 stats3 toutI2 finA0 normv3 finB0 toutI3 finA1 finB1"}
SCALE_FORM = "chunk"
SORT_SPLIT = 2
PROBE_LOADS_BEFORE = ()
FINAL_BY_GROUP = False
H_ON_SCALAR = ()
MX_ALIGN = 64
N_WARM = 0
SMALL_LOADS_BEFORE = 2
W_BEFORE_SCALES = True
CONST_BANKS = "turn"
RSQRT = True
PAIR_FROM = None
PAIR_TO = None
POOL_SCALES_FROM = None
PAIR_STARTS = ()
VECTOR_BANKS = ()
CODE_BUFS = 2
SORT_SPLITS = {}
WARM_BEFORE_TURN = {}
WARM_BEFORE_MULTIPLY = {}
FINAL_BY_HALF = False
SCALES_AHEAD = False
RELU_ON_VECTOR = ()
QUANT_BANKS = {1: 2, 2: 2, 3: 2, 4: 2, 5: 2, 6: 2, 7: 2, 8: 2, 9: 2, 10: 2, 11: 2, 12: 2, 13: 2, 14: 2}


def make_slabs():
    slabs = []
    if PAIR_FROM is not None:
        for chunk in range(PAIR_FROM):
            for b in range(BATCH):
                slabs.append(((IMAGE_TILES * b, IMAGE_TILES * b + 1), chunk * CHUNK_GROUPS, CHUNK_GROUPS))
        for chunk in range(PAIR_FROM, PAIR_TO, 2):
            for t in range(TILES):
                slabs.append(((t,), chunk * CHUNK_GROUPS, 2 * CHUNK_GROUPS))
        for chunk in range(PAIR_TO, CHUNKS):
            for b in range(BATCH):
                slabs.append(((IMAGE_TILES * b, IMAGE_TILES * b + 1), chunk * CHUNK_GROUPS, CHUNK_GROUPS))
        return slabs
    image_chunks = CHUNKS - TILE_END_CHUNKS
    for chunk in range(image_chunks):
        for b in range(BATCH):
            slabs.append(((IMAGE_TILES * b, IMAGE_TILES * b + 1), chunk * CHUNK_GROUPS, CHUNK_GROUPS))
    if TILE_END_CHUNKS:
        for t in range(TILES):
            slabs.append(((t,), image_chunks * CHUNK_GROUPS, TILE_END_CHUNKS * CHUNK_GROUPS))
    return slabs


def units_of_bank(i, slab, j):
    tiles, first, groups = slab
    if len(tiles) == SLOTS and i not in TILE_MAJOR:
        return [(t, first + j) for t in tiles]
    per_tile = BANKS // len(tiles)
    return [(tiles[j // per_tile], first + SLOTS * (j % per_tile) + s) for s in range(SLOTS)]


def tile_transformerconvblock_pc_k_kernel(
    tc, h, ffn2_w_words, ffn2_w_scales, ffn2_b, scale_ffn, ln2_w, ln2_b, scale_norm2, x, out
):
    nc = tc.nc
    h_view = h.flatten_outer_dims().rearrange("(t p) k -> p t k", p=P)
    w_view = ffn2_w_words.rearrange("g p n t -> p g (n t)")
    slabs = make_slabs()
    items = []
    for i in range(len(slabs)):
        parts = SPLITS.get(i, 1)
        step = BANKS // parts
        for a in range(parts):
            items.append((i, a * step, (a + 1) * step))
    n_items = len(items)

    with ExitStack() as ctx:
        ctx.enter_context(tc.manual_schedule())
        consts = ctx.enter_context(tc.tile_pool(name="consts", bufs=1))
        h_pool = ctx.enter_context(tc.tile_pool(name="h_pool", bufs=H_BUFS))
        w_pool = ctx.enter_context(tc.tile_pool(name="w_pool", bufs=W_BUFS))
        sort_pool = ctx.enter_context(tc.tile_pool(name="sort_pool", bufs=SORT_BUFS))
        work = ctx.enter_context(tc.tile_pool(name="work", bufs=2))
        code_pool = ctx.enter_context(tc.tile_pool(name="code_pool", bufs=CODE_BUFS))
        tail = ctx.enter_context(tc.tile_pool(name="tail", bufs=TILES))
        image_pool = ctx.enter_context(tc.tile_pool(name="image_pool", bufs=BATCH))
        acc_pool = ctx.enter_context(tc.psum_pool(name="acc_pool", bufs=1))
        turn_pool = ctx.enter_context(tc.psum_pool(name="turn_pool", bufs=4))

        one_row = consts.tile([P, CHANNELS + SCALAR_COLS], BF16)
        nc.vector.memset(one_row[:], 0.0)
        ln_rows = consts.tile([P, P], BF16)
        nc.vector.memset(ln_rows[:], 0.0)
        ffn_col = CHANNELS + FFN_SCALE_COL
        norm_col = CHANNELS + NORM_SCALE_COL

        def small_loads(queue):
            queue.dma_start(out=one_row[0:1, 0:CHANNELS], in_=ffn2_b.unsqueeze(0))
            queue.dma_start(out=one_row[0:1, ffn_col : ffn_col + 1], in_=scale_ffn.unsqueeze(0))
            queue.dma_start(out=one_row[0:1, norm_col : norm_col + 1], in_=scale_norm2.unsqueeze(0))
            queue.dma_start(out=ln_rows[0:CHANNEL_TILES, :], in_=ln2_w.rearrange("(j c) -> j c", c=P))
            queue.dma_start(
                out=ln_rows[CHANNEL_TILES : 2 * CHANNEL_TILES, :], in_=ln2_b.rearrange("(j c) -> j c", c=P)
            )

        if SMALL_LOADS_BEFORE is None:
            small_loads(nc.scalar)

        w_planes = consts.tile([P, CHUNKS, CHANNELS], U8, align_bytes=MX_ALIGN)
        nc.vector.memset(w_planes[:].bitcast(I32), 0)
        x_rows = consts.tile([P, BATCH, CHANNEL_TILES, IMAGE], BF16)

        plan = []
        planned = set()
        last_use = {}
        for k in range(n_items + 1):
            if k < n_items:
                plan.append(("h",) + items[k])
            if k >= 1:
                i, j0, j1 = items[k - 1]
                for j in range(j0, j1):
                    for t, g in units_of_bank(i, slabs[i], j):
                        chunk = g // CHUNK_GROUPS
                        last_use[chunk] = k - 1
                        pieces = W_PIECES.get(chunk, 1)
                        piece = (g % CHUNK_GROUPS) * pieces // CHUNK_GROUPS
                        if ("s", chunk) not in planned and not SCALES_FIRST and not W_BEFORE_SCALES:
                            planned.add(("s", chunk))
                            plan.append(("s", chunk))
                        if ("w", chunk, piece) not in planned:
                            planned.add(("w", chunk, piece))
                            plan.append(("w", chunk, piece))
                        if ("s", chunk) not in planned and not SCALES_FIRST:
                            planned.add(("s", chunk))
                            plan.append(("s", chunk))
        if SCALES_FIRST:
            where = [n for n, e in enumerate(plan) if e[0] == "w"][0] if SCALES_FIRST == "before W" else 0
            plan[where:where] = [("s", -1)]
        for chunk, slab in MOVES:
            moved = [e for e in plan if e[0] in ("s", "w") and e[1] == chunk]
            plan = [e for e in plan if e not in moved]
            where = [n for n, e in enumerate(plan) if e[0] == "h" and e[1] == slab][0]
            plan[where:where] = moved
        h_places = [n for n, e in enumerate(plan) if e[0] == "h"]
        for b in reversed(range(BATCH)):
            back = X_BEFORE[b]
            if back:
                plan[h_places[-back] : h_places[-back]] = [("x", b)]
            else:
                plan.append(("x", b))

        for n, slab in enumerate(PROBE_LOADS_BEFORE):
            where = [m for m, e in enumerate(plan) if e[0] == "h" and e[1] == slab][0]
            plan[where:where] = [("d", n)]
        if SMALL_LOADS_BEFORE is not None:
            plan[SMALL_LOADS_BEFORE:SMALL_LOADS_BEFORE] = [("c",)]
        if SCALES_AHEAD:
            for chunk in range(1, CHUNKS):
                plan.remove(("s", chunk))
                where = max(n for n, e in enumerate(plan) if e[0] == "h" and e[1] == 2 * chunk - 1)
                plan[where + 1 : where + 1] = [("s", chunk)]
        pool_scales = [e for e in plan if e[0] == "s" and POOL_SCALES_FROM is not None and e[1] >= POOL_SCALES_FROM]
        plan = [e for e in plan if e not in pool_scales]
        h_tiles = {}
        w_tiles = {}
        state = {"next": 0, "sorted": 0, "chunks": 0}

        def issue(entry):
            kind = entry[0]
            if kind == "h":
                i, j0, j1 = entry[1:]
                tiles, first, groups = slabs[i]
                if i not in h_tiles:
                    h_rows = h_pool.tile([P, SLAB_K], BF16, tag="h_rows")
                    h_tiles[i] = h_rows
                by_tile = h_tiles[i][:].rearrange("p (t k) -> p t k", t=len(tiles))
                width = SLAB_K // len(tiles)
                if len(tiles) == SLOTS and i not in TILE_MAJOR:
                    per_bank = width // BANKS
                    spans = [(0, len(tiles), j0 * per_bank, j1 * per_bank)]
                elif j1 - j0 == BANKS:
                    spans = [(0, len(tiles), 0, width)]
                else:
                    per_tile = BANKS // len(tiles)
                    per_bank = width // per_tile
                    assert j0 // per_tile == (j1 - 1) // per_tile
                    spans = [(j0 // per_tile, j0 // per_tile + 1, (j0 % per_tile) * per_bank, (j0 % per_tile + j1 - j0) * per_bank)]
                queue = nc.scalar if i in H_ON_SCALAR else nc.sync
                for t0, t1, k0, k1 in spans:
                    queue.dma_start(
                        out=by_tile[:, t0:t1, k0:k1],
                        in_=h_view[:, tiles[0] + t0 : tiles[0] + t1, first * K_PASS + k0 : first * K_PASS + k1],
                    )
            elif kind == "c":
                small_loads(nc.sync)
            elif kind == "d":
                probe = consts.tile([P, SLAB_K], BF16, name="probe%d" % entry[1])
                nc.sync.dma_start(
                    out=probe[:].rearrange("p (t k) -> p t k", t=SLOTS), in_=h_view[:, 0:SLOTS, 0 : SLAB_K // SLOTS]
                )
            elif kind == "s" and entry[1] < 0 and SCALE_FORM == "member":
                for member in range(CHUNK_GROUPS):
                    for quadrant in range(QUADRANTS):
                        first = 32 * quadrant + QUADRANT_SCALES * member
                        rows = slice(quadrant * QUADRANT_SCALES, (quadrant + 1) * QUADRANT_SCALES)
                        nc.sync.dma_start(
                            out=w_planes[first : first + QUADRANT_SCALES, :, :].bitcast(I32),
                            in_=ffn2_w_scales[member::CHUNK_GROUPS, rows, :].rearrange("a r n -> r a n").bitcast(I32),
                        )
            elif kind == "s" and entry[1] < 0 and SCALE_FORM == "quadrant":
                for quadrant in range(QUADRANTS):
                    first = 32 * quadrant
                    rows = slice(quadrant * QUADRANT_SCALES, (quadrant + 1) * QUADRANT_SCALES)
                    nc.sync.dma_start(
                        out=w_planes[first : first + CHUNK_GROUPS * QUADRANT_SCALES, :, :].bitcast(I32),
                        in_=ffn2_w_scales[:, rows, :].rearrange("(a m) r n -> m r a n", m=CHUNK_GROUPS).bitcast(I32),
                    )
            elif kind == "s" and entry[1] < 0:
                for chunk in range(CHUNKS):
                    issue(("s", chunk))
            elif kind == "s":
                chunk = entry[1]
                groups = slice(chunk * CHUNK_GROUPS, (chunk + 1) * CHUNK_GROUPS)
                on_pool = POOL_SCALES_FROM is not None and chunk >= POOL_SCALES_FROM
                for quadrant in range(QUADRANTS):
                    first = 32 * quadrant
                    rows = slice(quadrant * QUADRANT_SCALES, (quadrant + 1) * QUADRANT_SCALES)
                    (nc.gpsimd if on_pool else nc.sync).dma_start(
                        out=w_planes[first : first + CHUNK_GROUPS * QUADRANT_SCALES, chunk, :].bitcast(F32 if on_pool else I32),
                        in_=ffn2_w_scales[groups, rows, :].bitcast(F32 if on_pool else I32),
                    )
            elif kind == "w":
                chunk, piece = entry[1:]
                if chunk not in w_tiles:
                    w_words = w_pool.tile([P, CHUNK_GROUPS, PACK * CHANNELS], U8, tag="w_words", align_bytes=MX_ALIGN)
                    w_tiles[chunk] = w_words
                per = CHUNK_GROUPS // W_PIECES.get(chunk, 1)
                nc.sync.dma_start(
                    out=w_tiles[chunk][:, piece * per : (piece + 1) * per, :].bitcast(I32),
                    in_=w_view[
                        :, chunk * CHUNK_GROUPS + piece * per : chunk * CHUNK_GROUPS + (piece + 1) * per, :
                    ].bitcast(I32),
                )
            else:
                b = entry[1]
                nc.sync.dma_start(out=x_rows[:, b, :, :], in_=x[b].rearrange("(j c) i w -> c j (i w)", c=P))

        def pump():
            while state["next"] < len(plan):
                entry = plan[state["next"]]
                if entry[0] == "h" and entry[1] >= H_BUFS + state["sorted"]:
                    return
                if entry[0] == "w" and entry[1] >= W_BUFS + state["chunks"]:
                    return
                issue(entry)
                state["next"] += 1

        pump()

        ident_f32 = consts.tile([P, P], F32)
        make_identity(nc, ident_f32[:])
        ident_bf16 = consts.tile([P, P], BF16)
        make_identity(nc, ident_bf16[:])
        for entry in pool_scales:
            issue(entry)
        ones = consts.tile([P, P], BF16)
        nc.vector.memset(ones[:], 1.0)
        one_col = consts.tile([P, 1], F32)
        nc.vector.memset(one_col[:], 1.0)
        eps_col = consts.tile([P, 1], F32)
        nc.scalar.activation(out=eps_col[:], in_=one_col[:], func=ACT.Copy, scale=EPS)
        sqrt_warm = consts.tile([P, 1], F32)
        nc.scalar.activation(out=sqrt_warm[:], in_=one_col[:], func=ACT.Abs_reciprocal_sqrt if RSQRT else ACT.Sqrt)

        acc = {}
        warm_tiles = {}

        def warm(n):
            if not n:
                return
            if not warm_tiles:
                warm_in = consts.tile([P, CHANNELS], BF16)
                nc.vector.memset(warm_in[:], 0.0)
                warm_bank = acc_pool.tile([P, CHANNELS], F32, name="acc3")
                warm_tiles[0] = (warm_in, warm_bank)
            assert 3 not in acc
            for m in range(n):
                nc.tensor.matmul(out=warm_tiles[0][1][:], lhsT=ones[:], rhs=warm_tiles[0][0][:], start=True, stop=True)

        warm(N_WARM)

        bias_all = consts.tile([P, CHANNELS], F32)
        scalars = consts.tile([P, SCALAR_COLS], F32)
        ffn_scale = scalars[:, FFN_SCALE_COL : FFN_SCALE_COL + 1]
        norm_scale = scalars[:, NORM_SCALE_COL : NORM_SCALE_COL + 1]
        ffn_scale_sq = consts.tile([P, 1], F32)
        ln_cols = consts.tile([P, 2 * CHANNEL_TILES], F32)
        var_scale = consts.tile([P, 1], F32)

        def make_constants():
            if CONST_BANKS == "acc":
                assert 2 not in acc and 3 not in acc
                scalar_bank = acc_pool.tile([P, SCALAR_COLS], F32, name="acc2")
            else:
                scalar_bank = turn_pool.tile([P, SCALAR_COLS], F32, tag="turn")
            nc.tensor.matmul(
                out=scalar_bank[:], lhsT=ones[:], rhs=one_row[:, CHANNELS : CHANNELS + SCALAR_COLS], start=True, stop=True
            )
            nc.scalar.copy(out=scalars[:], in_=scalar_bank[:])
            if CONST_BANKS == "acc":
                bias_bank = acc_pool.tile([P, CHANNELS], F32, name="acc3")
            else:
                bias_bank = turn_pool.tile([P, CHANNELS], F32, tag="turn")
            nc.tensor.matmul(out=bias_bank[:], lhsT=ones[:], rhs=one_row[:, 0:CHANNELS], start=True, stop=True)
            nc.scalar.copy(out=bias_all[:], in_=bias_bank[:])
            nc.scalar.activation(out=ffn_scale_sq[:], in_=ffn_scale, func=ACT.Copy, scale=ffn_scale)
            nc.scalar.activation(out=var_scale[:], in_=ffn_scale_sq[:], func=ACT.Copy, scale=1.0 / CHANNELS)
            if CONST_BANKS == "acc":
                ln_bank = acc_pool.tile([P, P], BF16, name="acc2")
            else:
                ln_bank = turn_pool.tile([P, P], BF16, tag="turn")
            nc.tensor.transpose(ln_bank[:], ln_rows[:], ident_bf16[:])
            nc.scalar.activation(out=ln_cols[:], in_=ln_bank[:, 0 : 2 * CHANNEL_TILES], func=ACT.Copy, scale=norm_scale)
            nc.scalar.activation(
                out=ln_cols[:, 0:CHANNEL_TILES], in_=ln_cols[:, 0:CHANNEL_TILES], func=ACT.Copy, scale=ffn_scale
            )


        sorted_tiles = {}
        grouped_tiles = {}
        code_tiles = {}

        done = set()

        def sort(k):
            if ("sort", k) in done:
                return
            done.add(("sort", k))
            i, j0, j1 = items[k]
            tiles = slabs[i][0]
            if i not in sorted_tiles:
                sorted_words = sort_pool.tile([P, BANKS, SLOTS, HALVES, P], F32, tag="sorted_words")
                sorted_tiles[i] = sorted_words
            h_words = h_tiles[i][:].bitcast(F32)
            if len(tiles) == SLOTS and i not in TILE_MAJOR:
                per_bank = SLAB_K // SLOTS // BANKS // 2
                source = h_words.rearrange("p (s w) -> p s w", s=SLOTS)[:, :, j0 * per_bank : j1 * per_bank].rearrange(
                    "p s (j q u) -> p j s u q", j=j1 - j0, u=HALVES
                )
            else:
                per_bank = SLAB_K // BANKS // 2
                source = h_words[:, j0 * per_bank : j1 * per_bank].rearrange(
                    "p (j s q u) -> p j s u q", j=j1 - j0, s=SLOTS, u=HALVES
                )
            step = max(1, (j1 - j0) // SORT_SPLITS.get(i, SORT_SPLIT))
            for a in range(0, j1 - j0, step):
                nc.vector.tensor_copy(out=sorted_tiles[i][:, j0 + a : j0 + a + step, :, :, :], in_=source[:, a : a + step, :, :, :])
            if j1 == BANKS:
                h_tiles.pop(i)
                state["sorted"] += 1
                pump()

        def turn(k, by_vector=()):
            i, j0, j1 = items[k]
            if i not in grouped_tiles:
                grouped = work.tile([P, BANKS, IMAGE * PACK], BF16, tag="grouped", align_bytes=MX_ALIGN)
                grouped_tiles[i] = grouped
            grouped_words = grouped_tiles[i][:].bitcast(F32).rearrange("p j (x u) -> p j x u", u=HALVES)
            for j in range(j0, j1):
                turned = turn_pool.tile([P, HALVES, IMAGE], F32, tag="turn")
                for s in range(SLOTS):
                    for u in range(HALVES):
                        nc.tensor.transpose(turned[:, u, s * P : (s + 1) * P], sorted_tiles[i][:, j, s, u, :], ident_f32[:])
                if j in by_vector:
                    nc.vector.tensor_copy(out=grouped_words[:, j, :, :], in_=turned[:].rearrange("p u x -> p x u"))
                else:
                    nc.scalar.copy(out=grouped_words[:, j, :, :], in_=turned[:].rearrange("p u x -> p x u"))
            if j1 == BANKS:
                sorted_tiles.pop(i)

        def quantise(k):
            if ("quantise", k) in done:
                return
            done.add(("quantise", k))
            i, j0, j1 = items[k]
            if i not in code_tiles:
                h_codes = code_pool.tile([P, BANKS, IMAGE], U32, tag="h_codes", align_bytes=MX_ALIGN)
                h_planes = code_pool.tile([P, BANKS, IMAGE], U8, tag="h_planes", align_bytes=MX_ALIGN)
                code_tiles[i] = (h_codes, h_planes)
            h_codes, h_planes = code_tiles[i]
            step = QUANT_BANKS.get(i, 1) if j1 - j0 == BANKS else 1
            for j in range(j0, j1, step):
                nc.vector.quantize_mx(
                    out=h_codes[:, j : j + step, :].rearrange("p j x -> p (j x)").bitcast(FP8X4),
                    scales=h_planes[:, j : j + step, :].rearrange("p j x -> p (j x)"),
                    in_=grouped_tiles[i][:, j : j + step, :].rearrange("p j x -> p (j x)"),
                )
            if j1 == BANKS:
                grouped_tiles.pop(i)

        def multiply(k, banks=None):
            i, j0, j1 = items[k]
            h_codes, h_planes = code_tiles[i]
            for j in range(j0, j1) if banks is None else banks:
                for s, (t, g) in enumerate(units_of_bank(i, slabs[i], j)):
                    chunk, member = divmod(g, CHUNK_GROUPS)
                    pixels = slice(s * P, (s + 1) * P)
                    if t not in acc:
                        bank = acc_pool.tile([P, CHANNELS], F32, name="acc%d" % t)
                        acc[t] = bank
                    nc.tensor.matmul_mx(
                        out=acc[t][:],
                        lhsT=h_codes[:, j, pixels].bitcast(FP8X4),
                        lhsT_scale=h_planes[:, j, pixels],
                        rhs=w_tiles[chunk][:, member, :].bitcast(FP8X4),
                        rhs_scale=w_planes[QUADRANT_SCALES * member : P, chunk, :],
                        start=(g == 0),
                        stop=(g == GROUPS - 1),
                    )
            if banks is not None:
                return
            if j1 == BANKS:
                code_tiles.pop(i)
            freed = [chunk for chunk in last_use if last_use[chunk] == k]
            if freed:
                state["chunks"] += len(freed)
                pump()

        biased_tiles = {}
        mean_var_tiles = {}
        spread_tiles = {}
        gain_tiles = {}
        unit_tiles = {}
        turned_out = {}

        def bias(t):
            biased = tail.tile([P, CHANNELS], F32, tag="biased")
            nc.vector.tensor_tensor(out=biased[:], in0=acc[t][:], in1=bias_all[:], op=ALU.add)
            biased_tiles[t] = biased

        def stats(t):
            stat = tail.tile([P, 6], F32, tag="stat")
            nc.vector.bn_stats(out=stat[:], in_=biased_tiles[t][:])
            mean_var = tail.tile([P, 2], F32, tag="mean_var")
            nc.vector.bn_aggr(out=mean_var[:], in_=stat[:])
            spread = tail.tile([P, 1], F32, tag="spread")
            if RSQRT:
                nc.scalar.activation(
                    out=spread[:], in_=mean_var[:, 1:2], func=ACT.Abs_reciprocal_sqrt, scale=ffn_scale_sq[:], bias=eps_col[:]
                )
            else:
                nc.vector.tensor_scalar(
                    out=spread[:], in0=mean_var[:, 1:2], scalar1=ffn_scale_sq[:], scalar2=EPS, op0=ALU.mult, op1=ALU.add
                )
                nc.scalar.activation(out=spread[:], in_=spread[:], func=ACT.Sqrt)
            mean_var_tiles[t] = mean_var
            spread_tiles[t] = spread

        def normv(t):
            if RSQRT:
                gain = spread_tiles[t]
            else:
                gain = tail.tile([P, 1], F32, tag="gain")
                nc.vector.reciprocal(out=gain[:], in_=spread_tiles[t][:])
            unit = tail.tile([P, CHANNELS], F32, tag="unit")
            nc.vector.tensor_scalar(
                out=unit[:],
                in0=biased_tiles[t][:],
                scalar1=mean_var_tiles[t][:, 0:1],
                scalar2=gain[:],
                op0=ALU.subtract,
                op1=ALU.mult,
            )
            unit_tiles[t] = unit

        def gain(t):
            pair = tail.tile([P, 2], F32, tag="pair")
            nc.vector.reciprocal(out=pair[:, 0:1], in_=spread_tiles[t][:])
            nc.vector.scalar_tensor_tensor(
                out=pair[:, 1:2], in0=mean_var_tiles[t][:, 0:1], scalar=-1.0, in1=pair[:, 0:1], op0=ALU.mult, op1=ALU.mult
            )
            gain_tiles[t] = pair

        def norms(t):
            unit = tail.tile([P, CHANNELS], F32, tag="unit")
            nc.scalar.activation(
                out=unit[:], in_=biased_tiles[t][:], func=ACT.Identity, scale=gain_tiles[t][:, 0:1], bias=gain_tiles[t][:, 1:2]
            )
            unit_tiles[t] = unit

        def tout(t):
            turned = acc_pool.tile([P, CHANNEL_TILES, P], F32, name="acc%d" % t)
            for j in range(CHANNEL_TILES):
                nc.tensor.transpose(turned[:, j, :], unit_tiles[t][:, j * P : (j + 1) * P], ident_f32[:])
            turned_out[t] = turned

        def fin(t):
            b, half = divmod(t, IMAGE_TILES)
            pixels = slice(half * P, (half + 1) * P)
            out_view = out[b].rearrange("(j c) i w -> c j (i w)", c=P)
            summed = tail.tile([P, CHANNEL_TILES, P], F32, tag="summed")
            result = tail.tile([P, CHANNEL_TILES, P], F32, tag="result")
            for j in range(CHANNEL_TILES):
                nc.vector.scalar_tensor_tensor(
                    out=summed[:, j, :],
                    in0=turned_out[t][:, j, :],
                    scalar=ln_cols[:, j : j + 1],
                    in1=x_rows[:, b, j, pixels],
                    op0=ALU.mult,
                    op1=ALU.add,
                )
                nc.scalar.activation(
                    out=result[:, j, :],
                    in_=summed[:, j, :],
                    func=ACT.Relu,
                    bias=ln_cols[:, CHANNEL_TILES + j : CHANNEL_TILES + j + 1],
                )
                if j % STORE_EVERY == STORE_EVERY - 1:
                    js = slice(j + 1 - STORE_EVERY, j + 1)
                    nc.sync.dma_start(out=out_view[:, js, pixels], in_=result[:, js, :])

        sum_tiles = {}

        def biasS(t):
            biased = tail.tile([P, CHANNELS], F32, tag="biased")
            sums = tail.tile([P, 4], F32, tag="sums")
            nc.vector.scalar_tensor_tensor(
                out=biased[:], in0=acc[t][:], scalar=1.0, in1=bias_all[:], op0=ALU.mult, op1=ALU.add, accum_out=sums[:, 0:1]
            )
            biased_tiles[t] = biased
            sum_tiles[t] = sums

        def statsS(t):
            sums = sum_tiles[t]
            nc.scalar.activation(out=sums[:, 1:2], in_=sums[:, 0:1], func=ACT.Copy, scale=-1.0 / CHANNELS)
            squares = tail.tile([P, CHANNELS], F32, tag="unit")
            nc.scalar.activation(
                out=squares[:], in_=biased_tiles[t][:], func=ACT.Square, bias=sums[:, 1:2], accum_out=sums[:, 2:3]
            )
            if RSQRT:
                pair = tail.tile([P, 2], F32, tag="pair")
                nc.scalar.activation(
                    out=pair[:, 0:1], in_=sums[:, 2:3], func=ACT.Abs_reciprocal_sqrt, scale=var_scale[:], bias=eps_col[:]
                )
                nc.scalar.activation(out=pair[:, 1:2], in_=sums[:, 1:2], func=ACT.Copy, scale=pair[:, 0:1])
                gain_tiles[t] = pair
            else:
                nc.scalar.activation(out=sums[:, 3:4], in_=sums[:, 2:3], func=ACT.Sqrt, scale=var_scale[:], bias=eps_col[:])

        def gainS(t):
            if RSQRT:
                return
            sums = sum_tiles[t]
            pair = tail.tile([P, 2], F32, tag="pair")
            nc.vector.reciprocal(out=pair[:, 0:1], in_=sums[:, 3:4])
            nc.vector.tensor_tensor(out=pair[:, 1:2], in0=sums[:, 1:2], in1=pair[:, 0:1], op=ALU.mult)
            gain_tiles[t] = pair

        image_banks = {}

        def toutI(t):
            b, half = divmod(t, IMAGE_TILES)
            if b not in image_banks:
                bank_a = acc_pool.tile([P, 2, IMAGE], F32, name="acc%d" % (IMAGE_TILES * b))
                bank_b = acc_pool.tile([P, 2, IMAGE], F32, name="acc%d" % (IMAGE_TILES * b + 1))
                image_banks[b] = (bank_a, bank_b)
            for j in range(CHANNEL_TILES):
                nc.tensor.transpose(
                    image_banks[b][j // 2][:, j % 2, half * P : (half + 1) * P], unit_tiles[t][:, j * P : (j + 1) * P], ident_f32[:]
                )

        def finI(b):
            out_view = out[b].rearrange("(j c) i w -> c j (i w)", c=P)
            summed = image_pool.tile([P, CHANNEL_TILES, IMAGE], F32, tag="summedI")
            result = image_pool.tile([P, CHANNEL_TILES, IMAGE], F32, tag="resultI")
            for j in range(CHANNEL_TILES):
                nc.vector.scalar_tensor_tensor(
                    out=summed[:, j, :],
                    in0=image_banks[b][j // 2][:, j % 2, :],
                    scalar=ln_cols[:, j : j + 1],
                    in1=x_rows[:, b, j, :],
                    op0=ALU.mult,
                    op1=ALU.add,
                )
                nc.scalar.activation(
                    out=result[:, j, :],
                    in_=summed[:, j, :],
                    func=ACT.Relu,
                    bias=ln_cols[:, CHANNEL_TILES + j : CHANNEL_TILES + j + 1],
                )
                if j % STORE_EVERY == STORE_EVERY - 1:
                    js = slice(j + 1 - STORE_EVERY, j + 1)
                    nc.sync.dma_start(out=out_view[:, js, :], in_=result[:, js, :])

        def normV(t):
            unit = tail.tile([P, CHANNELS], F32, tag="unit")
            nc.vector.tensor_scalar(
                out=unit[:],
                in0=biased_tiles[t][:],
                scalar1=gain_tiles[t][:, 0:1],
                scalar2=gain_tiles[t][:, 1:2],
                op0=ALU.mult,
                op1=ALU.add,
            )
            unit_tiles[t] = unit

        last_tiles = {}

        def last_stage(b, js, pixels, store):
            if b not in last_tiles:
                summed = image_pool.tile([P, CHANNEL_TILES, IMAGE], F32, tag="summedI")
                result = image_pool.tile([P, CHANNEL_TILES, IMAGE], F32, tag="resultI")
                last_tiles[b] = (summed, result)
            summed, result = last_tiles[b]
            out_view = out[b].rearrange("(j c) i w -> c j (i w)", c=P)
            for j in js:
                nc.vector.scalar_tensor_tensor(
                    out=summed[:, j, pixels],
                    in0=image_banks[b][j // 2][:, j % 2, pixels],
                    scalar=ln_cols[:, j : j + 1],
                    in1=x_rows[:, b, j, pixels],
                    op0=ALU.mult,
                    op1=ALU.add,
                )
                if store and j in RELU_ON_VECTOR:
                    nc.vector.tensor_scalar(
                        out=result[:, j, pixels],
                        in0=summed[:, j, pixels],
                        scalar1=ln_cols[:, CHANNEL_TILES + j : CHANNEL_TILES + j + 1],
                        scalar2=0.0,
                        op0=ALU.add,
                        op1=ALU.max,
                    )
                else:
                    nc.scalar.activation(
                        out=result[:, j, pixels],
                        in_=summed[:, j, pixels],
                        func=ACT.Relu,
                        bias=ln_cols[:, CHANNEL_TILES + j : CHANNEL_TILES + j + 1],
                    )
                if store:
                    nc.sync.dma_start(out=out_view[:, j : j + 1, :], in_=result[:, j : j + 1, :])

        def finA(b):
            last_stage(b, (0, 1), slice(0, IMAGE), True)

        def finB(b):
            last_stage(b, (2, 3), slice(0, IMAGE), True)

        def finT(t):
            b, half = divmod(t, IMAGE_TILES)
            last_stage(b, range(CHANNEL_TILES), slice(half * P, (half + 1) * P), half == IMAGE_TILES - 1)

        stages = {"normV": normV, "finA": finA, "finB": finB, "finT": finT, "biasS": biasS, "statsS": statsS, "gainS": gainS, "toutI": toutI, "finI": finI, "bias": bias, "stats": stats, "normv": normv, "gain": gain, "norms": norms, "tout": tout, "fin": fin}

        def run(names):
            for name in names.split():
                stages[name[:-1]](int(name[-1]))

        sort(0)
        if CONST_AFTER < 0:
            make_constants()
        for k in range(n_items + 1):
            back = k - n_items
            if k - 1 in PAIR_STARTS:
                continue
            if k in PAIR_STARTS:
                turn(k, VECTOR_BANKS)
                turn(k + 1)
                quantise(k - 1)
                quantise(k)
                multiply(k - 1)
                if k + 2 < n_items:
                    sort(k + 2)
                quantise(k + 1)
                if k + 3 < n_items and k + 2 in PAIR_STARTS:
                    sort(k + 3)
                multiply(k)
                continue
            warm(WARM_BEFORE_TURN.get(k, 0))
            if k < n_items:
                turn(k)
            if k == CONST_AFTER:
                make_constants()
            run(AFTER_TURN.get(back, ""))
            if k >= 1:
                quantise(k - 1)
            if k + 1 < n_items:
                sort(k + 1)
            if k + 1 in PAIR_STARTS:
                sort(k + 2)
            run(AFTER_QUANTISE.get(back, ""))
            if k >= 1 and FINAL_BY_HALF and back == 0:
                for half in range(2):
                    for item in (k - 2, k - 1):
                        multiply(item, [half, 2 + half])
            elif k >= 1 and FINAL_BY_HALF and back == -1:
                pass
            elif k >= 1 and FINAL_BY_GROUP and back == 0:
                for j in range(BANKS):
                    multiply(k - 2, [j])
                    multiply(k - 1, [j])
            elif k >= 1 and not (FINAL_BY_GROUP and back == -1):
                warm(WARM_BEFORE_MULTIPLY.get(k - 1, 0))
                multiply(k - 1)
            run(AFTER_MULTIPLY.get(back, ""))
